import numpy as np
import ml_dtypes


def mxq(x, axis, fmt="e4m3"):
    dtype, down = {"e4m3": (ml_dtypes.float8_e4m3fn, 7), "e5m2": (ml_dtypes.float8_e5m2, 14)}[fmt]
    v = np.moveaxis(np.asarray(x, np.float32).astype(ml_dtypes.bfloat16).astype(np.float64), axis, -1)
    blocks = v.reshape(v.shape[:-1] + (-1, 32))
    amax = np.abs(blocks).max(-1, keepdims=True)
    byte = np.maximum(np.where(amax > 0, np.frexp(amax)[1] - 1 + 127, 0) - down, 1)
    scale = np.exp2(byte - 127.0)
    codes = (blocks / scale).astype(np.float32).astype(dtype).astype(np.float64)
    return np.moveaxis((codes * scale).reshape(v.shape), -1, axis)


WIDE = False


def mx_kscale(k):
    if not WIDE:
        return np.ones(k)
    levels = np.array([10, -10, 5, -5, 0])
    a = np.random.permutation(np.resize(levels, k // 512 * 4)).reshape(k // 512, 4)
    idx = np.arange(k)
    return np.exp2(a[idx // 512, idx % 128 // 32])


BF16 = ml_dtypes.bfloat16


def bf(x):
    return np.asarray(x, np.float32).astype(BF16)


def f64(x):
    return np.asarray(x).astype(np.float64)


B, N, C, DIM, H = 4, 1024, 512, 1024, 8
D = DIM // H // 2
LAYER_NUM = 12
LAM_INIT = 0.8 - 0.6 * np.exp(-0.3 * LAYER_NUM)
EPS = 1e-5


def setup_inputs():
    s = mx_kscale(C)
    sc = np.random.standard_normal((B, N, 2 * H, 2 * H))
    att = np.exp(sc) / np.exp(sc).sum(-1, keepdims=True)
    diff = att[:, :, :H, :H] - LAM_INIT * att[:, :, H:, H:]
    return {"x": bf(np.random.standard_normal((B, N, C)) * s),
            "diff": bf(diff),
            "Wv": bf(np.random.standard_normal((DIM, C)) * 0.02 * np.sqrt(H / C) / s),
            "Wo": bf(np.random.standard_normal((C, DIM)) * 2.0 / np.sqrt(DIM)),
            "bo": bf(np.random.standard_normal(C) * 0.1)}


def reference(x, diff, Wv, Wo, bo):
    v = (mxq(f64(x), 2, "e4m3") @ mxq(f64(Wv), 1, "e4m3").T).reshape(B, N, H, 2 * D)
    w = f64(diff)
    out = sum(w[:, :, :, h:h + 1] * v[:, :, h:h + 1, :] for h in range(H))
    out = out * (1.0 / np.sqrt(np.mean(out * out, axis=-1, keepdims=True) + EPS))
    out = out * (1.0 - LAM_INIT)
    out = out.reshape(B, N, DIM)
    return (mxq(out, 2, "e4m3") @ mxq(f64(Wo), 1, "e4m3").T) + f64(bo)

@@ -1,0 +1,204 @@
+import math
+from contextlib import ExitStack
+
+import concourse.mybir as mybir
+from concourse.masks import make_identity
+
+F32 = mybir.dt.float32
+BF16 = mybir.dt.bfloat16
+U32 = mybir.dt.uint32
+U8 = mybir.dt.uint8
+FP8X4 = mybir.dt.float8_e4m3fn_x4
+ACT = mybir.ActivationFunctionType
+ALU = mybir.AluOpType
+
+P = 128
+PACK = 4
+TOKENS = 4 * 1024
+C = 512
+DIM = 1024
+H = 8
+HD = DIM // H
+BANK = 512
+N_TILES = TOKENS // P
+PAIR = 2
+CHUNK = 4
+L0 = 0.8 - 0.6 * math.exp(-0.3 * 12)
+EPS = 1e-5
+
+FLOPS = 2 * TOKENS * C * DIM * 2 + 2 * TOKENS * H * H * HD
+
+
+def tile_differentialattention_pb_t_kernel(tc, x, diff, Wv, Wo, bo, out):
+    nc = tc.nc
+    x_view = x.flatten_outer_dims().rearrange("(p i) k -> p i k", i=N_TILES)
+    diff_view = diff.rearrange("b n a h -> (b n) (a h)").rearrange("(p i) c -> p i c", i=N_TILES)
+    out_view = out.flatten_outer_dims().rearrange("(p i) c -> p i c", i=N_TILES)
+
+    with ExitStack() as stack:
+        keep = stack.enter_context(tc.tile_pool(name="keep", bufs=1))
+        stage = stack.enter_context(tc.tile_pool(name="stage", bufs=4))
+        psum = stack.enter_context(tc.psum_pool(name="psum", bufs=1))
+
+        ident_f32 = keep.tile([P, P], F32)
+        make_identity(nc, ident_f32[:])
+        ident_bf16 = keep.tile([P, P], BF16)
+        make_identity(nc, ident_bf16[:])
+
+        wv_raw = keep.tile([P, DIM // P, C], BF16)
+        nc.sync.dma_start(out=wv_raw[:], in_=Wv.rearrange("(r p) k -> p r k", p=P))
+        diff_raw = keep.tile([P, N_TILES, H * H], BF16)
+        nc.sync.dma_start(out=diff_raw[:], in_=diff_view)
+        wo_raw = keep.tile([P, C // P, DIM], BF16)
+        nc.sync.dma_start(out=wo_raw[:], in_=Wo.rearrange("(r p) k -> p r k", p=P))
+        bias_raw = keep.tile([P, C], BF16)
+        nc.sync.dma_start(out=bias_raw[:], in_=bo.partition_broadcast(P))
+
+        weight = keep.tile([P, N_TILES, H * H], F32)
+        nc.vector.tensor_copy(out=weight[:], in_=diff_raw[:])
+        bias = keep.tile([P, C], F32)
+        nc.vector.tensor_copy(out=bias[:], in_=bias_raw[:])
+
+        wv_grouped = keep.tile([P, DIM, PACK], BF16, align_bytes=64)
+        wv_grouped_words = wv_grouped[:].rearrange("p w j -> p (w j)").bitcast(F32).rearrange(
+            "p (w u) -> p w u", u=2
+        )
+        for pair in range(DIM // P // PAIR):
+            wv_t = psum.tile([P, PAIR, 2, P], F32, tag="words_t")
+            for s in range(PAIR):
+                words = wv_raw[:, pair * PAIR + s, :].bitcast(F32)
+                for u in range(2):
+                    nc.tensor.transpose(wv_t[:, s, u, :], words[:, u * P : (u + 1) * P], ident_f32[:])
+            nc.vector.tensor_copy(
+                out=wv_grouped_words[:, pair * PAIR * P : (pair + 1) * PAIR * P, :].rearrange(
+                    "p (s w) u -> p s w u", s=PAIR
+                ),
+                in_=wv_t[:].rearrange("p s u w -> p s w u"),
+            )
+        wv_codes = keep.tile([P, DIM], U32, align_bytes=64)
+        wv_scales = keep.tile([P, DIM], U8, align_bytes=64)
+        nc.vector.quantize_mx(
+            out=wv_codes[:].bitcast(FP8X4),
+            scales=wv_scales[:],
+            in_=wv_grouped[:].rearrange("p w j -> p (w j)"),
+        )
+
+        wo_grouped = keep.tile([P, 2, C, PACK], BF16, align_bytes=64)
+        for r in range(C // P):
+            wo_t = psum.tile([P, H, P], BF16, tag="heads_t")
+            for a in range(H):
+                nc.tensor.transpose(wo_t[:, a, :], wo_raw[:, r, a * HD : (a + 1) * HD], ident_bf16[:])
+            nc.scalar.copy(
+                out=wo_grouped[:, :, r * P : (r + 1) * P, :],
+                in_=wo_t[:].rearrange("p (g j) c -> p g c j", j=PACK),
+            )
+        wo_codes = keep.tile([P, 2 * C], U32, align_bytes=64)
+        wo_scales = keep.tile([P, 2 * C], U8, align_bytes=64)
+        nc.vector.quantize_mx(
+            out=wo_codes[:].bitcast(FP8X4),
+            scales=wo_scales[:],
+            in_=wo_grouped[:].rearrange("p g c j -> p (g c j)"),
+        )
+
+        gain = 1.0 - L0
+
+        for i in range(N_TILES):
+            if i % CHUNK == 0:
+                x_raw = stage.tile([P, CHUNK, C], BF16)
+                nc.sync.dma_start(out=x_raw[:], in_=x_view[:, i : i + CHUNK, :])
+                out_sb = stage.tile([P, CHUNK, C], F32)
+
+            if i % PAIR == 0:
+                x_t = psum.tile([P, PAIR, 2, P], F32, tag="words_t")
+                for s in range(PAIR):
+                    words = x_raw[:, i % CHUNK + s, :].bitcast(F32)
+                    for u in range(2):
+                        nc.tensor.transpose(x_t[:, s, u, :], words[:, u * P : (u + 1) * P], ident_f32[:])
+                x_grouped = stage.tile([P, PAIR * P * PACK], BF16, align_bytes=64)
+                nc.scalar.copy(
+                    out=x_grouped[:].bitcast(F32).rearrange("p (s t u) -> p s t u", s=PAIR, u=2),
+                    in_=x_t[:].rearrange("p s u t -> p s t u"),
+                )
+                x_codes = stage.tile([P, PAIR * P], U32, align_bytes=64)
+                x_scales = stage.tile([P, PAIR * P], U8, align_bytes=64)
+                nc.vector.quantize_mx(out=x_codes[:].bitcast(FP8X4), scales=x_scales[:], in_=x_grouped[:])
+
+            tok = slice((i % PAIR) * P, (i % PAIR + 1) * P)
+            v_banks = []
+            for n in range(DIM // BANK):
+                v_bank = psum.tile([P, BANK], F32, tag="v%d" % n, bufs=2, name="v_bank")
+                nc.tensor.matmul_mx(
+                    out=v_bank[:],
+                    lhsT=x_codes[:, tok].bitcast(FP8X4),
+                    lhsT_scale=x_scales[:, tok],
+                    rhs=wv_codes[:, n * BANK : (n + 1) * BANK].bitcast(FP8X4),
+                    rhs_scale=wv_scales[:, n * BANK : (n + 1) * BANK],
+                    start=True,
+                    stop=True,
+                )
+                v_banks.append(v_bank)
+
+            def v_head(h):
+                per_bank = BANK // HD
+                return v_banks[h // per_bank][:, (h % per_bank) * HD : (h % per_bank + 1) * HD]
+
+            def w(a, h):
+                return weight[:, i, a * H + h : a * H + h + 1]
+
+            mix = stage.tile([P, H, HD], F32)
+            for a in range(H):
+                nc.scalar.activation(out=mix[:, a, :], in_=v_head(H - 1), func=ACT.Copy, scale=w(a, H - 1))
+            for h in range(H - 1):
+                for a in range(H):
+                    nc.vector.scalar_tensor_tensor(
+                        out=mix[:, a, :], in0=v_head(h), scalar=w(a, h), in1=mix[:, a, :],
+                        op0=ALU.mult, op1=ALU.add,
+                    )
+
+            sumsq = stage.tile([P, H], F32)
+            for a in range(H):
+                square = stage.tile([P, HD], BF16)
+                nc.scalar.activation(out=square[:], in_=mix[:, a, :], func=ACT.Square, accum_out=sumsq[:, a : a + 1])
+            meansq = stage.tile([P, H], F32)
+            nc.gpsimd.tensor_scalar(
+                out=meansq[:], in0=sumsq[:], scalar1=1.0 / (HD * gain * gain), scalar2=EPS / (gain * gain),
+                op0=ALU.mult, op1=ALU.add,
+            )
+            rms = stage.tile([P, H], F32)
+            nc.scalar.activation(out=rms[:], in_=meansq[:], func=ACT.Sqrt)
+            inv_rms = stage.tile([P, H], F32)
+            nc.vector.reciprocal(out=inv_rms[:], in_=rms[:])
+            r = stage.tile([P, H, HD], BF16)
+            nc.gpsimd.tensor_tensor(
+                out=r[:], in0=mix[:], in1=inv_rms[:].unsqueeze(2).to_broadcast([P, H, HD]), op=ALU.mult
+            )
+
+            r_t = psum.tile([P, H, P], BF16, tag="heads_t")
+            for a in range(H):
+                nc.tensor.transpose(r_t[:, a, :], r[:, a, :], ident_bf16[:])
+            r_grouped = stage.tile([P, 2, P, PACK], BF16, align_bytes=64)
+            nc.scalar.copy(out=r_grouped[:], in_=r_t[:].rearrange("p (g j) t -> p g t j", j=PACK))
+            r_codes = stage.tile([P, 2 * P], U32, align_bytes=64)
+            r_scales = stage.tile([P, 2 * P], U8, align_bytes=64)
+            nc.vector.quantize_mx(
+                out=r_codes[:].bitcast(FP8X4),
+                scales=r_scales[:],
+                in_=r_grouped[:].rearrange("p g t j -> p (g t j)"),
+            )
+
+            acc = psum.tile([P, C], F32, tag="acc")
+            for g in range(2):
+                nc.tensor.matmul_mx(
+                    out=acc[:],
+                    lhsT=r_codes[:, g * P : (g + 1) * P].bitcast(FP8X4),
+                    lhsT_scale=r_scales[:, g * P : (g + 1) * P],
+                    rhs=wo_codes[:, g * C : (g + 1) * C].bitcast(FP8X4),
+                    rhs_scale=wo_scales[:, g * C : (g + 1) * C],
+                    start=(g == 0),
+                    stop=(g == 1),
+                )
+            product = stage.tile([P, C], F32)
+            nc.scalar.copy(out=product[:], in_=acc[:])
+            nc.gpsimd.tensor_tensor(out=out_sb[:, i % CHUNK, :], in0=product[:], in1=bias[:], op=ALU.add)
+            if i % CHUNK == CHUNK - 1:
+                nc.sync.dma_start(out=out_view[:, i - CHUNK + 1 : i + 1, :], in_=out_sb[:])

@@ -11,6 +11,7 @@ U8 = mybir.dt.uint8
 FP8X4 = mybir.dt.float8_e4m3fn_x4
 ACT = mybir.ActivationFunctionType
 ALU = mybir.AluOpType
+AXIS = mybir.AxisListType
 
 P = 128
 PACK = 4
@@ -20,10 +21,20 @@ DIM = 1024
 H = 8
 HD = DIM // H
 BANK = 512
+HEADS_PER_BANK = BANK // HD
 N_TILES = TOKENS // P
+QUAD = 4
+N_QUADS = N_TILES // QUAD
+TENSOR_TILES = QUAD - 1
+N_SLOTS = N_QUADS * TENSOR_TILES
 PAIR = 2
-CHUNK = 4
+GROUP = P // H
+GROUPS = P // GROUP
+PARKING_SLOTS = 4
+PARKED = 2 * PARKING_SLOTS
+FIRST_PARKED = N_TILES - PARKED
 L0 = 0.8 - 0.6 * math.exp(-0.3 * 12)
+GAIN = 1.0 - L0
 EPS = 1e-5
 
 FLOPS = 2 * TOKENS * C * DIM * 2 + 2 * TOKENS * H * H * HD
@@ -31,14 +42,14 @@ FLOPS = 2 * TOKENS * C * DIM * 2 + 2 * TOKENS * H * H * HD
 
 def tile_differentialattention_pb_t_kernel(tc, x, diff, Wv, Wo, bo, out):
     nc = tc.nc
-    x_view = x.flatten_outer_dims().rearrange("(p i) k -> p i k", i=N_TILES)
-    diff_view = diff.rearrange("b n a h -> (b n) (a h)").rearrange("(p i) c -> p i c", i=N_TILES)
-    out_view = out.flatten_outer_dims().rearrange("(p i) c -> p i c", i=N_TILES)
+    x_rows = x.flatten_outer_dims()
+    diff_rows = diff.rearrange("b n a h -> (b n) (a h)")
+    out_rows = out.flatten_outer_dims()
 
     with ExitStack() as stack:
         keep = stack.enter_context(tc.tile_pool(name="keep", bufs=1))
-        stage = stack.enter_context(tc.tile_pool(name="stage", bufs=4))
-        psum = stack.enter_context(tc.psum_pool(name="psum", bufs=1))
+        stage = stack.enter_context(tc.tile_pool(name="stage", bufs=3))
+        psum = stack.enter_context(tc.psum_pool(name="psum", bufs=3))
 
         ident_f32 = keep.tile([P, P], F32)
         make_identity(nc, ident_f32[:])
@@ -47,45 +58,55 @@ def tile_differentialattention_pb_t_kernel(tc, x, diff, Wv, Wo, bo, out):
 
         wv_raw = keep.tile([P, DIM // P, C], BF16)
         nc.sync.dma_start(out=wv_raw[:], in_=Wv.rearrange("(r p) k -> p r k", p=P))
-        diff_raw = keep.tile([P, N_TILES, H * H], BF16)
-        nc.sync.dma_start(out=diff_raw[:], in_=diff_view)
-        wo_raw = keep.tile([P, C // P, DIM], BF16)
-        nc.sync.dma_start(out=wo_raw[:], in_=Wo.rearrange("(r p) k -> p r k", p=P))
-        bias_raw = keep.tile([P, C], BF16)
-        nc.sync.dma_start(out=bias_raw[:], in_=bo.partition_broadcast(P))
 
-        weight = keep.tile([P, N_TILES, H * H], F32)
-        nc.vector.tensor_copy(out=weight[:], in_=diff_raw[:])
-        bias = keep.tile([P, C], F32)
-        nc.vector.tensor_copy(out=bias[:], in_=bias_raw[:])
-
-        wv_grouped = keep.tile([P, DIM, PACK], BF16, align_bytes=64)
-        wv_grouped_words = wv_grouped[:].rearrange("p w j -> p (w j)").bitcast(F32).rearrange(
-            "p (w u) -> p w u", u=2
-        )
+        wv_grouped = keep.tile([P, DIM * PACK], BF16, align_bytes=64)
+        wv_grouped_words = wv_grouped[:].bitcast(F32).rearrange("p (s w u) -> p s w u", w=P, u=2)
         for pair in range(DIM // P // PAIR):
-            wv_t = psum.tile([P, PAIR, 2, P], F32, tag="words_t")
+            wv_t = psum.tile([P, PAIR, 2, P], F32, tag="misc")
             for s in range(PAIR):
                 words = wv_raw[:, pair * PAIR + s, :].bitcast(F32)
                 for u in range(2):
                     nc.tensor.transpose(wv_t[:, s, u, :], words[:, u * P : (u + 1) * P], ident_f32[:])
             nc.vector.tensor_copy(
-                out=wv_grouped_words[:, pair * PAIR * P : (pair + 1) * PAIR * P, :].rearrange(
-                    "p (s w) u -> p s w u", s=PAIR
-                ),
+                out=wv_grouped_words[:, pair * PAIR : (pair + 1) * PAIR],
                 in_=wv_t[:].rearrange("p s u w -> p s w u"),
             )
         wv_codes = keep.tile([P, DIM], U32, align_bytes=64)
         wv_scales = keep.tile([P, DIM], U8, align_bytes=64)
-        nc.vector.quantize_mx(
-            out=wv_codes[:].bitcast(FP8X4),
-            scales=wv_scales[:],
-            in_=wv_grouped[:].rearrange("p w j -> p (w j)"),
+        nc.vector.quantize_mx(out=wv_codes[:].bitcast(FP8X4), scales=wv_scales[:], in_=wv_grouped[:])
+
+        vector_diff_raw = keep.tile([P, N_QUADS, H * H], BF16)
+        nc.sync.dma_start(
+            out=vector_diff_raw[:],
+            in_=diff_rows.rearrange("(q s p) c -> p q s c", s=QUAD, p=P)[:, :, QUAD - 1, :],
+        )
+        vector_diff = keep.tile([P, N_QUADS, H * H], F32)
+        nc.vector.tensor_copy(out=vector_diff[:], in_=vector_diff_raw[:])
+
+        diff_groups = keep.tile([P, 2, GROUP * H * H], BF16)
+        nc.sync.dma_start(out=diff_groups[:], in_=diff_rows.rearrange("(y g t) c -> g y (t c)", y=2, t=GROUP))
+        diff_by_a = keep.tile([P, 2, H, GROUP, H], BF16)
+        head_weight = keep.tile([P, 2 * P, H], F32)
+        for y in range(2):
+            nc.vector.tensor_copy(
+                out=diff_by_a[:, y], in_=diff_groups[:, y, :].rearrange("p (t a h) -> p a t h", a=H, h=H)
+            )
+            diff_t = psum.tile([P, H, P], BF16, tag="misc")
+            for a in range(H):
+                nc.tensor.transpose(
+                    diff_t[:, a, :], diff_by_a[:, y, a].rearrange("p t h -> p (t h)"), ident_bf16[:]
+                )
+            nc.scalar.copy(out=head_weight[:, y * P : (y + 1) * P, :], in_=diff_t[:].rearrange("p a g -> p g a"))
+        same_token = keep.tile([P, GROUP], F32)
+        nc.vector.tensor_reduce(
+            out=same_token[:], in_=ident_f32[:].rearrange("p (t h) -> p t h", h=H), axis=AXIS.X, op=ALU.add
         )
 
+        wo_raw = keep.tile([P, C // P, DIM], BF16)
+        nc.sync.dma_start(out=wo_raw[:], in_=Wo.rearrange("(r p) k -> p r k", p=P))
         wo_grouped = keep.tile([P, 2, C, PACK], BF16, align_bytes=64)
         for r in range(C // P):
-            wo_t = psum.tile([P, H, P], BF16, tag="heads_t")
+            wo_t = psum.tile([P, H, P], BF16, tag="misc")
             for a in range(H):
                 nc.tensor.transpose(wo_t[:, a, :], wo_raw[:, r, a * HD : (a + 1) * HD], ident_bf16[:])
             nc.scalar.copy(
@@ -100,105 +121,232 @@ def tile_differentialattention_pb_t_kernel(tc, x, diff, Wv, Wo, bo, out):
             in_=wo_grouped[:].rearrange("p g c j -> p (g c j)"),
         )
 
-        gain = 1.0 - L0
+        bias_raw = keep.tile([P, C], BF16)
+        nc.sync.dma_start(out=bias_raw[:], in_=bo.partition_broadcast(P))
+        bias = keep.tile([P, C], F32)
+        nc.vector.tensor_copy(out=bias[:], in_=bias_raw[:])
 
-        for i in range(N_TILES):
-            if i % CHUNK == 0:
-                x_raw = stage.tile([P, CHUNK, C], BF16)
-                nc.sync.dma_start(out=x_raw[:], in_=x_view[:, i : i + CHUNK, :])
-                out_sb = stage.tile([P, CHUNK, C], F32)
+        eps_term = keep.tile([P, 1], F32)
+        nc.vector.tensor_scalar(
+            out=eps_term[:], in0=ident_f32[:, 0:1], scalar1=0.0, scalar2=EPS / (GAIN * GAIN), op0=ALU.mult, op1=ALU.add
+        )
 
-            if i % PAIR == 0:
-                x_t = psum.tile([P, PAIR, 2, P], F32, tag="words_t")
+        out_held = keep.tile([P, PARKED, C], F32)
+
+        x_raw = {}
+        x_codes = {}
+        parked = {}
+        vector_v = {}
+        vector_mix = {}
+        normed = {}
+        r_codes = {}
+
+        def load_x(q):
+            x_raw[q] = stage.tile([P, QUAD, C], BF16, name="x_raw")
+            nc.sync.dma_start(
+                out=x_raw[q][:], in_=x_rows[q * QUAD * P : (q + 1) * QUAD * P, :].rearrange("(s p) k -> p s k", p=P)
+            )
+
+        def quantise_x(q):
+            grouped = stage.tile([P, QUAD * P * PACK], BF16, align_bytes=64, name="x_grouped")
+            grouped_words = grouped[:].bitcast(F32).rearrange("p (s t u) -> p s t u", t=P, u=2)
+            for pair in range(QUAD // PAIR):
+                x_t = psum.tile([P, PAIR, 2, P], F32, tag="misc")
                 for s in range(PAIR):
-                    words = x_raw[:, i % CHUNK + s, :].bitcast(F32)
+                    words = x_raw[q][:, pair * PAIR + s, :].bitcast(F32)
                     for u in range(2):
                         nc.tensor.transpose(x_t[:, s, u, :], words[:, u * P : (u + 1) * P], ident_f32[:])
-                x_grouped = stage.tile([P, PAIR * P * PACK], BF16, align_bytes=64)
                 nc.scalar.copy(
-                    out=x_grouped[:].bitcast(F32).rearrange("p (s t u) -> p s t u", s=PAIR, u=2),
-                    in_=x_t[:].rearrange("p s u t -> p s t u"),
+                    out=grouped_words[:, pair * PAIR : (pair + 1) * PAIR], in_=x_t[:].rearrange("p s u t -> p s t u")
                 )
-                x_codes = stage.tile([P, PAIR * P], U32, align_bytes=64)
-                x_scales = stage.tile([P, PAIR * P], U8, align_bytes=64)
-                nc.vector.quantize_mx(out=x_codes[:].bitcast(FP8X4), scales=x_scales[:], in_=x_grouped[:])
+            codes = stage.tile([P, QUAD * P], U32, align_bytes=64, name="x_codes")
+            scales = stage.tile([P, QUAD * P], U8, align_bytes=64, name="x_scales")
+            nc.vector.quantize_mx(out=codes[:].bitcast(FP8X4), scales=scales[:], in_=grouped[:])
+            x_codes[q] = (codes, scales)
 
-            tok = slice((i % PAIR) * P, (i % PAIR + 1) * P)
-            v_banks = []
-            for n in range(DIM // BANK):
-                v_bank = psum.tile([P, BANK], F32, tag="v%d" % n, bufs=2, name="v_bank")
-                nc.tensor.matmul_mx(
-                    out=v_bank[:],
-                    lhsT=x_codes[:, tok].bitcast(FP8X4),
-                    lhsT_scale=x_scales[:, tok],
-                    rhs=wv_codes[:, n * BANK : (n + 1) * BANK].bitcast(FP8X4),
-                    rhs_scale=wv_scales[:, n * BANK : (n + 1) * BANK],
-                    start=True,
-                    stop=True,
+        def project_v(i, bank, v_bank):
+            codes, scales = x_codes[i // QUAD]
+            tok = slice((i % QUAD) * P, (i % QUAD + 1) * P)
+            cols = slice(bank * BANK, (bank + 1) * BANK)
+            nc.tensor.matmul_mx(
+                out=v_bank,
+                lhsT=codes[:, tok].bitcast(FP8X4),
+                lhsT_scale=scales[:, tok],
+                rhs=wv_codes[:, cols].bitcast(FP8X4),
+                rhs_scale=wv_scales[:, cols],
+                start=True,
+                stop=True,
+            )
+
+        def inverse_rms(sumsq, count):
+            rms = stage.tile([P, count], F32, name="rms")
+            nc.scalar.activation(
+                out=rms[:], in_=sumsq[:], func=ACT.Sqrt, scale=1.0 / (HD * GAIN * GAIN), bias=eps_term[:]
+            )
+            inv_rms = stage.tile([P, count], F32, name="inv_rms")
+            nc.vector.reciprocal(out=inv_rms[:], in_=rms[:])
+            return inv_rms
+
+        def sum_of_squares(values, total):
+            square = stage.tile([P, HD], BF16, name="square")
+            nc.scalar.activation(out=square[:], in_=values, func=ACT.Square, accum_out=total)
+
+        def park_heads(i, slot):
+            v_sb = stage.tile([P, DIM], F32, name="v_sb")
+            for bank in range(DIM // BANK):
+                v_bank = psum.tile([P, BANK], F32, tag="misc")
+                project_v(i, bank, v_bank[:])
+                copy_out = (nc.vector.tensor_copy, nc.scalar.copy)[bank]
+                copy_out(out=v_sb[:, bank * BANK : (bank + 1) * BANK], in_=v_bank[:])
+            first_row = (FIRST_PARKED + 2 * (slot % PARKING_SLOTS)) * P
+            space = out_rows[first_row : first_row + 2 * P, :].rearrange("r c -> (r c)")
+            nc.sync.dma_start(out=space.rearrange("(t w) -> t w", t=P), in_=v_sb[:])
+            v_heads = stage.tile([P, GROUPS, HD], F32, name="v_heads", bufs=4)
+            nc.sync.dma_start(out=v_heads[:], in_=space.rearrange("(g p d) -> p g d", g=GROUPS, p=P))
+            blocks = stage.tile([P, GROUPS, GROUP, H], F32, name="blocks", bufs=4)
+            nc.gpsimd.tensor_tensor(
+                out=blocks[:],
+                in0=head_weight[:, i * GROUPS : (i + 1) * GROUPS, :].unsqueeze(2).to_broadcast([P, GROUPS, GROUP, H]),
+                in1=same_token[:].unsqueeze(1).unsqueeze(3).to_broadcast([P, GROUPS, GROUP, H]),
+                op=ALU.mult,
+            )
+            parked[i] = (v_heads, blocks)
+
+        def mix_on_tensor(i):
+            v_heads, blocks = parked[i]
+            r = stage.tile([P, GROUPS, HD], BF16, name="r")
+            for bank in range(GROUPS // HEADS_PER_BANK):
+                mix_bank = psum.tile([P, HEADS_PER_BANK, HD], F32, tag="mix")
+                for s in range(HEADS_PER_BANK):
+                    g = bank * HEADS_PER_BANK + s
+                    nc.tensor.matmul(
+                        out=mix_bank[:, s, :],
+                        lhsT=blocks[:, g].rearrange("p t a -> p (t a)"),
+                        rhs=v_heads[:, g, :],
+                        start=True,
+                        stop=True,
+                    )
+                sumsq = stage.tile([P, HEADS_PER_BANK], F32, name="sumsq")
+                for s in range(HEADS_PER_BANK):
+                    sum_of_squares(mix_bank[:, s, :], sumsq[:, s : s + 1])
+                inv_rms = inverse_rms(sumsq, HEADS_PER_BANK)
+                nc.vector.tensor_tensor(
+                    out=r[:, bank * HEADS_PER_BANK : (bank + 1) * HEADS_PER_BANK, :],
+                    in0=mix_bank[:],
+                    in1=inv_rms[:].unsqueeze(2).to_broadcast([P, HEADS_PER_BANK, HD]),
+                    op=ALU.mult,
                 )
-                v_banks.append(v_bank)
+            normed[i] = (r, "p (t q j) -> p q t j")
 
-            def v_head(h):
-                per_bank = BANK // HD
-                return v_banks[h // per_bank][:, (h % per_bank) * HD : (h % per_bank + 1) * HD]
+        def vector_weight(q, a, h):
+            return vector_diff[:, q, a * H + h : a * H + h + 1]
 
-            def w(a, h):
-                return weight[:, i, a * H + h : a * H + h + 1]
+        def vector_head(q, h):
+            col = (h % HEADS_PER_BANK) * HD
+            return vector_v[(q, h // HEADS_PER_BANK)][:, col : col + HD]
 
-            mix = stage.tile([P, H, HD], F32)
-            for a in range(H):
-                nc.scalar.activation(out=mix[:, a, :], in_=v_head(H - 1), func=ACT.Copy, scale=w(a, H - 1))
-            for h in range(H - 1):
+        def vector_project(q, bank):
+            vector_v[(q, bank)] = psum.tile([P, BANK], F32, tag="vector_v%d" % bank, bufs=1, name="vector_v")
+            project_v(q * QUAD + QUAD - 1, bank, vector_v[(q, bank)][:])
+
+        def vector_start(q):
+            vector_project(q, 1)
+            products = stage.tile([P, 2, H, HD], F32, name="products", bufs=2)
+            for s in range(2):
+                for a in range(H):
+                    nc.scalar.activation(
+                        out=products[:, s, a, :], in_=vector_head(q, H - 2 + s), func=ACT.Copy,
+                        scale=vector_weight(q, a, H - 2 + s),
+                    )
+            vector_mix[q] = stage.tile([P, H, HD], F32, name="vector_mix", bufs=2)
+            nc.gpsimd.tensor_tensor(out=vector_mix[q][:], in0=products[:, 0], in1=products[:, 1], op=ALU.add)
+
+        def vector_add_heads(q, heads):
+            mix = vector_mix[q]
+            for h in heads:
                 for a in range(H):
                     nc.vector.scalar_tensor_tensor(
-                        out=mix[:, a, :], in0=v_head(h), scalar=w(a, h), in1=mix[:, a, :],
+                        out=mix[:, a, :], in0=vector_head(q, h), scalar=vector_weight(q, a, h), in1=mix[:, a, :],
                         op0=ALU.mult, op1=ALU.add,
                     )
 
-            sumsq = stage.tile([P, H], F32)
+        def vector_norm(q):
+            mix = vector_mix[q]
+            sumsq = stage.tile([P, H], F32, name="sumsq")
             for a in range(H):
-                square = stage.tile([P, HD], BF16)
-                nc.scalar.activation(out=square[:], in_=mix[:, a, :], func=ACT.Square, accum_out=sumsq[:, a : a + 1])
-            meansq = stage.tile([P, H], F32)
-            nc.gpsimd.tensor_scalar(
-                out=meansq[:], in0=sumsq[:], scalar1=1.0 / (HD * gain * gain), scalar2=EPS / (gain * gain),
-                op0=ALU.mult, op1=ALU.add,
-            )
-            rms = stage.tile([P, H], F32)
-            nc.scalar.activation(out=rms[:], in_=meansq[:], func=ACT.Sqrt)
-            inv_rms = stage.tile([P, H], F32)
-            nc.vector.reciprocal(out=inv_rms[:], in_=rms[:])
-            r = stage.tile([P, H, HD], BF16)
+                sum_of_squares(mix[:, a, :], sumsq[:, a : a + 1])
+            inv_rms = inverse_rms(sumsq, H)
+            r = stage.tile([P, H, HD], BF16, name="r")
             nc.gpsimd.tensor_tensor(
                 out=r[:], in0=mix[:], in1=inv_rms[:].unsqueeze(2).to_broadcast([P, H, HD]), op=ALU.mult
             )
+            normed[q * QUAD + QUAD - 1] = (r, "p (q j t) -> p q t j")
 
-            r_t = psum.tile([P, H, P], BF16, tag="heads_t")
-            for a in range(H):
-                nc.tensor.transpose(r_t[:, a, :], r[:, a, :], ident_bf16[:])
-            r_grouped = stage.tile([P, 2, P, PACK], BF16, align_bytes=64)
-            nc.scalar.copy(out=r_grouped[:], in_=r_t[:].rearrange("p (g j) t -> p g t j", j=PACK))
-            r_codes = stage.tile([P, 2 * P], U32, align_bytes=64)
-            r_scales = stage.tile([P, 2 * P], U8, align_bytes=64)
+        def quantise_r(i):
+            r, regroup = normed[i]
+            r_t = psum.tile([P, H, P], BF16, tag="misc")
+            for s in range(H):
+                nc.tensor.transpose(r_t[:, s, :], r[:, s, :], ident_bf16[:])
+            grouped = stage.tile([P, 2, P, PACK], BF16, align_bytes=64, name="r_grouped")
+            nc.scalar.copy(out=grouped[:], in_=r_t[:].rearrange("p s c -> p (s c)").rearrange(regroup, q=2, j=PACK))
+            codes = stage.tile([P, 2 * P], U32, align_bytes=64, name="r_codes")
+            scales = stage.tile([P, 2 * P], U8, align_bytes=64, name="r_scales")
             nc.vector.quantize_mx(
-                out=r_codes[:].bitcast(FP8X4),
-                scales=r_scales[:],
-                in_=r_grouped[:].rearrange("p g t j -> p (g t j)"),
+                out=codes[:].bitcast(FP8X4), scales=scales[:], in_=grouped[:].rearrange("p q t j -> p (q t j)")
             )
+            r_codes[i] = (codes, scales)
 
-            acc = psum.tile([P, C], F32, tag="acc")
+        def project_out(i):
+            codes, scales = r_codes[i]
+            acc = psum.tile([P, C], F32, tag="misc")
             for g in range(2):
                 nc.tensor.matmul_mx(
                     out=acc[:],
-                    lhsT=r_codes[:, g * P : (g + 1) * P].bitcast(FP8X4),
-                    lhsT_scale=r_scales[:, g * P : (g + 1) * P],
+                    lhsT=codes[:, g * P : (g + 1) * P].bitcast(FP8X4),
+                    lhsT_scale=scales[:, g * P : (g + 1) * P],
                     rhs=wo_codes[:, g * C : (g + 1) * C].bitcast(FP8X4),
                     rhs_scale=wo_scales[:, g * C : (g + 1) * C],
                     start=(g == 0),
                     stop=(g == 1),
                 )
-            product = stage.tile([P, C], F32)
+            product = stage.tile([P, C], F32, name="product")
             nc.scalar.copy(out=product[:], in_=acc[:])
-            nc.gpsimd.tensor_tensor(out=out_sb[:, i % CHUNK, :], in0=product[:], in1=bias[:], op=ALU.add)
-            if i % CHUNK == CHUNK - 1:
-                nc.sync.dma_start(out=out_view[:, i - CHUNK + 1 : i + 1, :], in_=out_sb[:])
+            if i < FIRST_PARKED:
+                out_sb = stage.tile([P, C], F32, name="out_sb")
+                nc.gpsimd.tensor_tensor(out=out_sb[:], in0=product[:], in1=bias[:], op=ALU.add)
+                nc.sync.dma_start(out=out_rows[i * P : (i + 1) * P, :], in_=out_sb[:])
+            else:
+                nc.gpsimd.tensor_tensor(out=out_held[:, i - FIRST_PARKED, :], in0=product[:], in1=bias[:], op=ALU.add)
+
+        def tensor_tile(k):
+            return (k // TENSOR_TILES) * QUAD + k % TENSOR_TILES
+
+        for k in range(-2 * TENSOR_TILES, N_SLOTS + 2 * TENSOR_TILES):
+            q, s = divmod(k, TENSOR_TILES)
+            if s == 0 and 0 <= q + 2 < N_QUADS:
+                load_x(q + 2)
+            if s == 0 and 0 <= q + 1 < N_QUADS:
+                quantise_x(q + 1)
+            if 0 <= k - 4 < N_SLOTS:
+                project_out(tensor_tile(k - 4))
+            if s == 2 and 0 <= q - 1 < N_QUADS:
+                project_out((q - 1) * QUAD + QUAD - 1)
+            if 0 <= k - 3 < N_SLOTS:
+                quantise_r(tensor_tile(k - 3))
+            if s == 1 and 0 <= q - 1 < N_QUADS:
+                quantise_r((q - 1) * QUAD + QUAD - 1)
+            if 0 <= k - 2 < N_SLOTS:
+                mix_on_tensor(tensor_tile(k - 2))
+            if s == 0 and 0 <= q - 1 < N_QUADS:
+                vector_norm(q - 1)
+            if 0 <= k < N_SLOTS:
+                park_heads(tensor_tile(k), k)
+            if s == 0 and 0 <= q < N_QUADS:
+                vector_project(q, 0)
+            if s == 1 and 0 <= q + 1 < N_QUADS:
+                vector_start(q + 1)
+            if 0 <= q < N_QUADS:
+                vector_add_heads(q, ((4, 5), (0, 1), (2, 3))[s])
+
+        for i in range(FIRST_PARKED, N_TILES):
+            nc.sync.dma_start(out=out_rows[i * P : (i + 1) * P, :], in_=out_held[:, i - FIRST_PARKED, :])

@@ -31,8 +31,7 @@ PAIR = 2
 GROUP = P // H
 GROUPS = P // GROUP
 PARKING_SLOTS = 4
-PARKED = 2 * PARKING_SLOTS
-FIRST_PARKED = N_TILES - PARKED
+FIRST_PARKED = N_TILES - 2 * PARKING_SLOTS
 L0 = 0.8 - 0.6 * math.exp(-0.3 * 12)
 GAIN = 1.0 - L0
 EPS = 1e-5
@@ -50,96 +49,104 @@ def tile_differentialattention_pb_t_kernel(tc, x, diff, Wv, Wo, bo, out):
         keep = stack.enter_context(tc.tile_pool(name="keep", bufs=1))
         stage = stack.enter_context(tc.tile_pool(name="stage", bufs=3))
         psum = stack.enter_context(tc.psum_pool(name="psum", bufs=3))
+        stack.enter_context(tc.manual_schedule())
+
+        wv_raw = keep.tile([P, DIM // P, C], BF16)
+        nc.sync.dma_start(out=wv_raw[:], in_=Wv.rearrange("(r p) k -> p r k", p=P))
+        vector_diff_raw = keep.tile([P, N_QUADS, H * H], BF16)
+        diff_groups = keep.tile([P, 2, GROUP * H * H], BF16)
+        wo_raw = keep.tile([P, C // P, DIM], BF16)
+        bias_raw = keep.tile([P, C], BF16)
+
+        def load_diff():
+            nc.sync.dma_start(
+                out=vector_diff_raw[:],
+                in_=diff_rows.rearrange("(q s p) c -> p q s c", s=QUAD, p=P)[:, :, QUAD - 1, :],
+            )
+            nc.sync.dma_start(out=diff_groups[:], in_=diff_rows.rearrange("(y g t) c -> g y (t c)", y=2, t=GROUP))
+
+        def load_wo():
+            nc.sync.dma_start(out=wo_raw[:], in_=Wo.rearrange("(r p) k -> p r k", p=P))
+            nc.sync.dma_start(out=bias_raw[:], in_=bo.partition_broadcast(P))
 
         ident_f32 = keep.tile([P, P], F32)
         make_identity(nc, ident_f32[:])
         ident_bf16 = keep.tile([P, P], BF16)
         make_identity(nc, ident_bf16[:])
-
-        wv_raw = keep.tile([P, DIM // P, C], BF16)
-        nc.sync.dma_start(out=wv_raw[:], in_=Wv.rearrange("(r p) k -> p r k", p=P))
-
-        wv_grouped = keep.tile([P, DIM * PACK], BF16, align_bytes=64)
-        wv_grouped_words = wv_grouped[:].bitcast(F32).rearrange("p (s w u) -> p s w u", w=P, u=2)
-        for pair in range(DIM // P // PAIR):
-            wv_t = psum.tile([P, PAIR, 2, P], F32, tag="misc")
-            for s in range(PAIR):
-                words = wv_raw[:, pair * PAIR + s, :].bitcast(F32)
-                for u in range(2):
-                    nc.tensor.transpose(wv_t[:, s, u, :], words[:, u * P : (u + 1) * P], ident_f32[:])
-            nc.vector.tensor_copy(
-                out=wv_grouped_words[:, pair * PAIR : (pair + 1) * PAIR],
-                in_=wv_t[:].rearrange("p s u w -> p s w u"),
-            )
-        wv_codes = keep.tile([P, DIM], U32, align_bytes=64)
-        wv_scales = keep.tile([P, DIM], U8, align_bytes=64)
-        nc.vector.quantize_mx(out=wv_codes[:].bitcast(FP8X4), scales=wv_scales[:], in_=wv_grouped[:])
-
-        vector_diff_raw = keep.tile([P, N_QUADS, H * H], BF16)
-        nc.sync.dma_start(
-            out=vector_diff_raw[:],
-            in_=diff_rows.rearrange("(q s p) c -> p q s c", s=QUAD, p=P)[:, :, QUAD - 1, :],
+        eps_term = keep.tile([P, 1], F32)
+        nc.vector.tensor_scalar(
+            out=eps_term[:], in0=ident_f32[:, 0:1], scalar1=0.0, scalar2=EPS / (GAIN * GAIN), op0=ALU.mult, op1=ALU.add
         )
-        vector_diff = keep.tile([P, N_QUADS, H * H], F32)
-        nc.vector.tensor_copy(out=vector_diff[:], in_=vector_diff_raw[:])
-
-        diff_groups = keep.tile([P, 2, GROUP * H * H], BF16)
-        nc.sync.dma_start(out=diff_groups[:], in_=diff_rows.rearrange("(y g t) c -> g y (t c)", y=2, t=GROUP))
-        diff_by_a = keep.tile([P, 2, H, GROUP, H], BF16)
-        head_weight = keep.tile([P, 2 * P, H], F32)
-        for y in range(2):
-            nc.vector.tensor_copy(
-                out=diff_by_a[:, y], in_=diff_groups[:, y, :].rearrange("p (t a h) -> p a t h", a=H, h=H)
-            )
-            diff_t = psum.tile([P, H, P], BF16, tag="misc")
-            for a in range(H):
-                nc.tensor.transpose(
-                    diff_t[:, a, :], diff_by_a[:, y, a].rearrange("p t h -> p (t h)"), ident_bf16[:]
-                )
-            nc.scalar.copy(out=head_weight[:, y * P : (y + 1) * P, :], in_=diff_t[:].rearrange("p a g -> p g a"))
         same_token = keep.tile([P, GROUP], F32)
         nc.vector.tensor_reduce(
             out=same_token[:], in_=ident_f32[:].rearrange("p (t h) -> p t h", h=H), axis=AXIS.X, op=ALU.add
         )
 
-        wo_raw = keep.tile([P, C // P, DIM], BF16)
-        nc.sync.dma_start(out=wo_raw[:], in_=Wo.rearrange("(r p) k -> p r k", p=P))
-        wo_grouped = keep.tile([P, 2, C, PACK], BF16, align_bytes=64)
-        for r in range(C // P):
-            wo_t = psum.tile([P, H, P], BF16, tag="misc")
-            for a in range(H):
-                nc.tensor.transpose(wo_t[:, a, :], wo_raw[:, r, a * HD : (a + 1) * HD], ident_bf16[:])
-            nc.scalar.copy(
-                out=wo_grouped[:, :, r * P : (r + 1) * P, :],
-                in_=wo_t[:].rearrange("p (g j) c -> p g c j", j=PACK),
-            )
+        wv_codes = keep.tile([P, DIM], U32, align_bytes=64)
+        wv_scales = keep.tile([P, DIM], U8, align_bytes=64)
         wo_codes = keep.tile([P, 2 * C], U32, align_bytes=64)
         wo_scales = keep.tile([P, 2 * C], U8, align_bytes=64)
-        nc.vector.quantize_mx(
-            out=wo_codes[:].bitcast(FP8X4),
-            scales=wo_scales[:],
-            in_=wo_grouped[:].rearrange("p g c j -> p (g c j)"),
-        )
-
-        bias_raw = keep.tile([P, C], BF16)
-        nc.sync.dma_start(out=bias_raw[:], in_=bo.partition_broadcast(P))
+        vector_diff = keep.tile([P, N_QUADS, H * H], F32)
+        head_weight = keep.tile([P, 2 * P, H], F32)
         bias = keep.tile([P, C], F32)
-        nc.vector.tensor_copy(out=bias[:], in_=bias_raw[:])
 
-        eps_term = keep.tile([P, 1], F32)
-        nc.vector.tensor_scalar(
-            out=eps_term[:], in0=ident_f32[:, 0:1], scalar1=0.0, scalar2=EPS / (GAIN * GAIN), op0=ALU.mult, op1=ALU.add
-        )
+        def prepare_wv():
+            grouped = keep.tile([P, DIM * PACK], BF16, align_bytes=64, name="wv_grouped")
+            grouped_words = grouped[:].bitcast(F32).rearrange("p (s w u) -> p s w u", w=P, u=2)
+            for pair in range(DIM // P // PAIR):
+                wv_t = psum.tile([P, PAIR, 2, P], F32, tag="misc")
+                for s in range(PAIR):
+                    words = wv_raw[:, pair * PAIR + s, :].bitcast(F32)
+                    for u in range(2):
+                        nc.tensor.transpose(wv_t[:, s, u, :], words[:, u * P : (u + 1) * P], ident_f32[:])
+                nc.vector.tensor_copy(
+                    out=grouped_words[:, pair * PAIR : (pair + 1) * PAIR], in_=wv_t[:].rearrange("p s u w -> p s w u")
+                )
+            nc.vector.quantize_mx(out=wv_codes[:].bitcast(FP8X4), scales=wv_scales[:], in_=grouped[:])
 
-        out_held = keep.tile([P, PARKED, C], F32)
+        def prepare_diff():
+            nc.vector.tensor_copy(out=vector_diff[:], in_=vector_diff_raw[:])
+            diff_by_a = keep.tile([P, 2, H, GROUP, H], BF16)
+            for y in range(2):
+                nc.vector.tensor_copy(
+                    out=diff_by_a[:, y], in_=diff_groups[:, y, :].rearrange("p (t a h) -> p a t h", a=H, h=H)
+                )
+                diff_t = psum.tile([P, H, P], BF16, tag="misc")
+                for a in range(H):
+                    nc.tensor.transpose(
+                        diff_t[:, a, :], diff_by_a[:, y, a].rearrange("p t h -> p (t h)"), ident_bf16[:]
+                    )
+                nc.scalar.copy(out=head_weight[:, y * P : (y + 1) * P, :], in_=diff_t[:].rearrange("p a g -> p g a"))
+
+        def prepare_wo():
+            grouped = keep.tile([P, 2, C, PACK], BF16, align_bytes=64, name="wo_grouped")
+            for r in range(C // P):
+                wo_t = psum.tile([P, H, P], BF16, tag="misc")
+                for a in range(H):
+                    nc.tensor.transpose(wo_t[:, a, :], wo_raw[:, r, a * HD : (a + 1) * HD], ident_bf16[:])
+                nc.scalar.copy(
+                    out=grouped[:, :, r * P : (r + 1) * P, :], in_=wo_t[:].rearrange("p (g j) c -> p g c j", j=PACK)
+                )
+            nc.vector.quantize_mx(
+                out=wo_codes[:].bitcast(FP8X4), scales=wo_scales[:], in_=grouped[:].rearrange("p g c j -> p (g c j)")
+            )
+            nc.vector.tensor_copy(out=bias[:], in_=bias_raw[:])
 
         x_raw = {}
+        x_grouped = {}
         x_codes = {}
-        parked = {}
+        v_heads = {}
+        blocks = {}
+        mix_banks = {}
+        rms = {}
         vector_v = {}
+        products = {}
         vector_mix = {}
-        normed = {}
+        r = {}
+        r_grouped = {}
         r_codes = {}
+        acc = {}
+        out_sb = {}
 
         def load_x(q):
             x_raw[q] = stage.tile([P, QUAD, C], BF16, name="x_raw")
@@ -147,21 +154,23 @@ def tile_differentialattention_pb_t_kernel(tc, x, diff, Wv, Wo, bo, out):
                 out=x_raw[q][:], in_=x_rows[q * QUAD * P : (q + 1) * QUAD * P, :].rearrange("(s p) k -> p s k", p=P)
             )
 
+        def transpose_x(q, pair):
+            if pair == 0:
+                x_grouped[q] = stage.tile([P, QUAD * P * PACK], BF16, align_bytes=64, name="x_grouped", bufs=2)
+            grouped_words = x_grouped[q][:].bitcast(F32).rearrange("p (s t u) -> p s t u", t=P, u=2)
+            x_t = psum.tile([P, PAIR, 2, P], F32, tag="misc")
+            for s in range(PAIR):
+                words = x_raw[q][:, pair * PAIR + s, :].bitcast(F32)
+                for u in range(2):
+                    nc.tensor.transpose(x_t[:, s, u, :], words[:, u * P : (u + 1) * P], ident_f32[:])
+            nc.scalar.copy(
+                out=grouped_words[:, pair * PAIR : (pair + 1) * PAIR], in_=x_t[:].rearrange("p s u t -> p s t u")
+            )
+
         def quantise_x(q):
-            grouped = stage.tile([P, QUAD * P * PACK], BF16, align_bytes=64, name="x_grouped")
-            grouped_words = grouped[:].bitcast(F32).rearrange("p (s t u) -> p s t u", t=P, u=2)
-            for pair in range(QUAD // PAIR):
-                x_t = psum.tile([P, PAIR, 2, P], F32, tag="misc")
-                for s in range(PAIR):
-                    words = x_raw[q][:, pair * PAIR + s, :].bitcast(F32)
-                    for u in range(2):
-                        nc.tensor.transpose(x_t[:, s, u, :], words[:, u * P : (u + 1) * P], ident_f32[:])
-                nc.scalar.copy(
-                    out=grouped_words[:, pair * PAIR : (pair + 1) * PAIR], in_=x_t[:].rearrange("p s u t -> p s t u")
-                )
             codes = stage.tile([P, QUAD * P], U32, align_bytes=64, name="x_codes")
             scales = stage.tile([P, QUAD * P], U8, align_bytes=64, name="x_scales")
-            nc.vector.quantize_mx(out=codes[:].bitcast(FP8X4), scales=scales[:], in_=grouped[:])
+            nc.vector.quantize_mx(out=codes[:].bitcast(FP8X4), scales=scales[:], in_=x_grouped[q][:])
             x_codes[q] = (codes, scales)
 
         def project_v(i, bank, v_bank):
@@ -178,65 +187,75 @@ def tile_differentialattention_pb_t_kernel(tc, x, diff, Wv, Wo, bo, out):
                 stop=True,
             )
 
-        def inverse_rms(sumsq, count):
-            rms = stage.tile([P, count], F32, name="rms")
+        def root_mean_square(values, count):
+            sumsq = stage.tile([P, count], F32, name="sumsq")
+            for s in range(count):
+                square = stage.tile([P, HD], BF16, name="square")
+                nc.scalar.activation(out=square[:], in_=values[:, s, :], func=ACT.Square, accum_out=sumsq[:, s : s + 1])
+            root = stage.tile([P, count], F32, name="root", bufs=4)
             nc.scalar.activation(
-                out=rms[:], in_=sumsq[:], func=ACT.Sqrt, scale=1.0 / (HD * GAIN * GAIN), bias=eps_term[:]
+                out=root[:], in_=sumsq[:], func=ACT.Sqrt, scale=1.0 / (HD * GAIN * GAIN), bias=eps_term[:]
             )
-            inv_rms = stage.tile([P, count], F32, name="inv_rms")
-            nc.vector.reciprocal(out=inv_rms[:], in_=rms[:])
-            return inv_rms
+            return root
 
-        def sum_of_squares(values, total):
-            square = stage.tile([P, HD], BF16, name="square")
-            nc.scalar.activation(out=square[:], in_=values, func=ACT.Square, accum_out=total)
+        def reciprocal(root, count):
+            inv = stage.tile([P, count], F32, name="inv", bufs=6)
+            nc.vector.reciprocal(out=inv[:], in_=root[:])
+            return inv[:].unsqueeze(2).to_broadcast([P, count, HD])
 
-        def park_heads(i, slot):
+        def parking_space(k):
+            first_row = (FIRST_PARKED + 2 * (k % PARKING_SLOTS)) * P
+            return out_rows[first_row : first_row + 2 * P, :].rearrange("r c -> (r c)")
+
+        def project_and_park(i, k):
             v_sb = stage.tile([P, DIM], F32, name="v_sb")
             for bank in range(DIM // BANK):
                 v_bank = psum.tile([P, BANK], F32, tag="misc")
                 project_v(i, bank, v_bank[:])
-                copy_out = (nc.vector.tensor_copy, nc.scalar.copy)[bank]
-                copy_out(out=v_sb[:, bank * BANK : (bank + 1) * BANK], in_=v_bank[:])
-            first_row = (FIRST_PARKED + 2 * (slot % PARKING_SLOTS)) * P
-            space = out_rows[first_row : first_row + 2 * P, :].rearrange("r c -> (r c)")
-            nc.sync.dma_start(out=space.rearrange("(t w) -> t w", t=P), in_=v_sb[:])
-            v_heads = stage.tile([P, GROUPS, HD], F32, name="v_heads", bufs=4)
-            nc.sync.dma_start(out=v_heads[:], in_=space.rearrange("(g p d) -> p g d", g=GROUPS, p=P))
-            blocks = stage.tile([P, GROUPS, GROUP, H], F32, name="blocks", bufs=4)
+                nc.vector.tensor_copy(out=v_sb[:, bank * BANK : (bank + 1) * BANK], in_=v_bank[:])
+            nc.sync.dma_start(out=parking_space(k).rearrange("(t w) -> t w", t=P), in_=v_sb[:])
+
+        def fetch_heads(i, k):
+            v_heads[i] = stage.tile([P, GROUPS, HD], F32, name="v_heads", bufs=5)
+            nc.sync.dma_start(out=v_heads[i][:], in_=parking_space(k).rearrange("(g p d) -> p g d", g=GROUPS, p=P))
+
+        def build_blocks(i):
+            blocks[i] = stage.tile([P, GROUPS, GROUP, H], F32, name="blocks", bufs=5)
             nc.gpsimd.tensor_tensor(
-                out=blocks[:],
+                out=blocks[i][:],
                 in0=head_weight[:, i * GROUPS : (i + 1) * GROUPS, :].unsqueeze(2).to_broadcast([P, GROUPS, GROUP, H]),
                 in1=same_token[:].unsqueeze(1).unsqueeze(3).to_broadcast([P, GROUPS, GROUP, H]),
                 op=ALU.mult,
             )
-            parked[i] = (v_heads, blocks)
 
         def mix_on_tensor(i):
-            v_heads, blocks = parked[i]
-            r = stage.tile([P, GROUPS, HD], BF16, name="r")
             for bank in range(GROUPS // HEADS_PER_BANK):
-                mix_bank = psum.tile([P, HEADS_PER_BANK, HD], F32, tag="mix")
+                mix_banks[(i, bank)] = psum.tile([P, HEADS_PER_BANK, HD], F32, tag="mix", name="mix_bank")
                 for s in range(HEADS_PER_BANK):
                     g = bank * HEADS_PER_BANK + s
                     nc.tensor.matmul(
-                        out=mix_bank[:, s, :],
-                        lhsT=blocks[:, g].rearrange("p t a -> p (t a)"),
-                        rhs=v_heads[:, g, :],
+                        out=mix_banks[(i, bank)][:, s, :],
+                        lhsT=blocks[i][:, g].rearrange("p t a -> p (t a)"),
+                        rhs=v_heads[i][:, g, :],
                         start=True,
                         stop=True,
                     )
-                sumsq = stage.tile([P, HEADS_PER_BANK], F32, name="sumsq")
-                for s in range(HEADS_PER_BANK):
-                    sum_of_squares(mix_bank[:, s, :], sumsq[:, s : s + 1])
-                inv_rms = inverse_rms(sumsq, HEADS_PER_BANK)
-                nc.vector.tensor_tensor(
-                    out=r[:, bank * HEADS_PER_BANK : (bank + 1) * HEADS_PER_BANK, :],
-                    in0=mix_bank[:],
-                    in1=inv_rms[:].unsqueeze(2).to_broadcast([P, HEADS_PER_BANK, HD]),
-                    op=ALU.mult,
-                )
-            normed[i] = (r, "p (t q j) -> p q t j")
+
+        def measure(i, bank):
+            rms[(i, bank)] = root_mean_square(mix_banks[(i, bank)], HEADS_PER_BANK)
+
+        def normalise(i, bank):
+            if bank == 0:
+                r[i] = stage.tile([P, GROUPS, HD], BF16, name="r", bufs=4)
+            nc.vector.tensor_tensor(
+                out=r[i][:, bank * HEADS_PER_BANK : (bank + 1) * HEADS_PER_BANK, :],
+                in0=mix_banks[(i, bank)][:],
+                in1=reciprocal(rms[(i, bank)], HEADS_PER_BANK),
+                op=ALU.mult,
+            )
+
+        def vector_tile(q):
+            return q * QUAD + QUAD - 1
 
         def vector_weight(q, a, h):
             return vector_diff[:, q, a * H + h : a * H + h + 1]
@@ -247,61 +266,62 @@ def tile_differentialattention_pb_t_kernel(tc, x, diff, Wv, Wo, bo, out):
 
         def vector_project(q, bank):
             vector_v[(q, bank)] = psum.tile([P, BANK], F32, tag="vector_v%d" % bank, bufs=1, name="vector_v")
-            project_v(q * QUAD + QUAD - 1, bank, vector_v[(q, bank)][:])
+            project_v(vector_tile(q), bank, vector_v[(q, bank)][:])
 
-        def vector_start(q):
-            vector_project(q, 1)
-            products = stage.tile([P, 2, H, HD], F32, name="products", bufs=2)
-            for s in range(2):
-                for a in range(H):
-                    nc.scalar.activation(
-                        out=products[:, s, a, :], in_=vector_head(q, H - 2 + s), func=ACT.Copy,
-                        scale=vector_weight(q, a, H - 2 + s),
-                    )
-            vector_mix[q] = stage.tile([P, H, HD], F32, name="vector_mix", bufs=2)
-            nc.gpsimd.tensor_tensor(out=vector_mix[q][:], in0=products[:, 0], in1=products[:, 1], op=ALU.add)
+        def vector_products(q, h):
+            if h == H - 2:
+                products[q] = stage.tile([P, 2, H, HD], F32, name="products", bufs=2)
+            for a in range(H):
+                nc.scalar.activation(
+                    out=products[q][:, h - (H - 2), a, :], in_=vector_head(q, h), func=ACT.Copy,
+                    scale=vector_weight(q, a, h),
+                )
+
+        def vector_join(q):
+            vector_mix[q] = stage.tile([P, H, HD], F32, name="vector_mix")
+            nc.gpsimd.tensor_tensor(out=vector_mix[q][:], in0=products[q][:, 0], in1=products[q][:, 1], op=ALU.add)
 
         def vector_add_heads(q, heads):
-            mix = vector_mix[q]
             for h in heads:
                 for a in range(H):
                     nc.vector.scalar_tensor_tensor(
-                        out=mix[:, a, :], in0=vector_head(q, h), scalar=vector_weight(q, a, h), in1=mix[:, a, :],
-                        op0=ALU.mult, op1=ALU.add,
+                        out=vector_mix[q][:, a, :], in0=vector_head(q, h), scalar=vector_weight(q, a, h),
+                        in1=vector_mix[q][:, a, :], op0=ALU.mult, op1=ALU.add,
                     )
 
-        def vector_norm(q):
-            mix = vector_mix[q]
-            sumsq = stage.tile([P, H], F32, name="sumsq")
-            for a in range(H):
-                sum_of_squares(mix[:, a, :], sumsq[:, a : a + 1])
-            inv_rms = inverse_rms(sumsq, H)
-            r = stage.tile([P, H, HD], BF16, name="r")
-            nc.gpsimd.tensor_tensor(
-                out=r[:], in0=mix[:], in1=inv_rms[:].unsqueeze(2).to_broadcast([P, H, HD]), op=ALU.mult
-            )
-            normed[q * QUAD + QUAD - 1] = (r, "p (q j t) -> p q t j")
+        def vector_measure(q):
+            rms[vector_tile(q)] = root_mean_square(vector_mix[q], H)
+
+        def vector_normalise(q):
+            i = vector_tile(q)
+            r[i] = stage.tile([P, H, HD], BF16, name="r", bufs=4)
+            nc.gpsimd.tensor_tensor(out=r[i][:], in0=vector_mix[q][:], in1=reciprocal(rms[i], H), op=ALU.mult)
+
+        def transpose_r(i):
+            r_t = psum.tile([P, H * P], BF16, tag="misc")
+            for s in range(H):
+                nc.tensor.transpose(r_t[:, s * P : (s + 1) * P], r[i][:, s, :], ident_bf16[:])
+            if i % QUAD == QUAD - 1:
+                by_pass = r_t[:].rearrange("p (q j t) -> p q t j", q=2, j=PACK)
+            else:
+                by_pass = r_t[:].rearrange("p (t q j) -> p q t j", q=2, j=PACK)
+            r_grouped[i] = stage.tile([P, 2, P, PACK], BF16, align_bytes=64, name="r_grouped")
+            nc.scalar.copy(out=r_grouped[i][:], in_=by_pass)
 
         def quantise_r(i):
-            r, regroup = normed[i]
-            r_t = psum.tile([P, H, P], BF16, tag="misc")
-            for s in range(H):
-                nc.tensor.transpose(r_t[:, s, :], r[:, s, :], ident_bf16[:])
-            grouped = stage.tile([P, 2, P, PACK], BF16, align_bytes=64, name="r_grouped")
-            nc.scalar.copy(out=grouped[:], in_=r_t[:].rearrange("p s c -> p (s c)").rearrange(regroup, q=2, j=PACK))
             codes = stage.tile([P, 2 * P], U32, align_bytes=64, name="r_codes")
             scales = stage.tile([P, 2 * P], U8, align_bytes=64, name="r_scales")
             nc.vector.quantize_mx(
-                out=codes[:].bitcast(FP8X4), scales=scales[:], in_=grouped[:].rearrange("p q t j -> p (q t j)")
+                out=codes[:].bitcast(FP8X4), scales=scales[:], in_=r_grouped[i][:].rearrange("p q t j -> p (q t j)")
             )
             r_codes[i] = (codes, scales)
 
         def project_out(i):
             codes, scales = r_codes[i]
-            acc = psum.tile([P, C], F32, tag="misc")
+            acc[i] = psum.tile([P, C], F32, tag="misc", name="acc")
             for g in range(2):
                 nc.tensor.matmul_mx(
-                    out=acc[:],
+                    out=acc[i][:],
                     lhsT=codes[:, g * P : (g + 1) * P].bitcast(FP8X4),
                     lhsT_scale=scales[:, g * P : (g + 1) * P],
                     rhs=wo_codes[:, g * C : (g + 1) * C].bitcast(FP8X4),
@@ -309,44 +329,96 @@ def tile_differentialattention_pb_t_kernel(tc, x, diff, Wv, Wo, bo, out):
                     start=(g == 0),
                     stop=(g == 1),
                 )
-            product = stage.tile([P, C], F32, name="product")
-            nc.scalar.copy(out=product[:], in_=acc[:])
-            if i < FIRST_PARKED:
-                out_sb = stage.tile([P, C], F32, name="out_sb")
-                nc.gpsimd.tensor_tensor(out=out_sb[:], in0=product[:], in1=bias[:], op=ALU.add)
-                nc.sync.dma_start(out=out_rows[i * P : (i + 1) * P, :], in_=out_sb[:])
-            else:
-                nc.gpsimd.tensor_tensor(out=out_held[:, i - FIRST_PARKED, :], in0=product[:], in1=bias[:], op=ALU.add)
+
+        def add_bias(i):
+            product = stage.tile([P, C], F32, name="product", bufs=4)
+            nc.scalar.copy(out=product[:], in_=acc[i][:])
+            out_sb[i] = stage.tile([P, C], F32, name="out_sb", bufs=6)
+            nc.gpsimd.tensor_tensor(out=out_sb[i][:], in0=product[:], in1=bias[:], op=ALU.add)
+
+        def store_out(i, k):
+            assert i < FIRST_PARKED or k > N_SLOTS - PARKING_SLOTS + (i - FIRST_PARKED) // 2 + 1
+            nc.sync.dma_start(out=out_rows[i * P : (i + 1) * P, :], in_=out_sb[i][:])
 
         def tensor_tile(k):
             return (k // TENSOR_TILES) * QUAD + k % TENSOR_TILES
 
-        for k in range(-2 * TENSOR_TILES, N_SLOTS + 2 * TENSOR_TILES):
-            q, s = divmod(k, TENSOR_TILES)
-            if s == 0 and 0 <= q + 2 < N_QUADS:
-                load_x(q + 2)
-            if s == 0 and 0 <= q + 1 < N_QUADS:
-                quantise_x(q + 1)
-            if 0 <= k - 4 < N_SLOTS:
-                project_out(tensor_tile(k - 4))
-            if s == 2 and 0 <= q - 1 < N_QUADS:
-                project_out((q - 1) * QUAD + QUAD - 1)
-            if 0 <= k - 3 < N_SLOTS:
-                quantise_r(tensor_tile(k - 3))
-            if s == 1 and 0 <= q - 1 < N_QUADS:
-                quantise_r((q - 1) * QUAD + QUAD - 1)
-            if 0 <= k - 2 < N_SLOTS:
-                mix_on_tensor(tensor_tile(k - 2))
-            if s == 0 and 0 <= q - 1 < N_QUADS:
-                vector_norm(q - 1)
-            if 0 <= k < N_SLOTS:
-                park_heads(tensor_tile(k), k)
-            if s == 0 and 0 <= q < N_QUADS:
-                vector_project(q, 0)
-            if s == 1 and 0 <= q + 1 < N_QUADS:
-                vector_start(q + 1)
-            if 0 <= q < N_QUADS:
-                vector_add_heads(q, ((4, 5), (0, 1), (2, 3))[s])
+        def is_slot(k):
+            return 0 <= k < N_SLOTS
 
-        for i in range(FIRST_PARKED, N_TILES):
-            nc.sync.dma_start(out=out_rows[i * P : (i + 1) * P, :], in_=out_held[:, i - FIRST_PARKED, :])
+        def is_quad(q):
+            return 0 <= q < N_QUADS
+
+        def slot(k):
+            q, s = divmod(k, TENSOR_TILES)
+            if is_slot(k - 6):
+                add_bias(tensor_tile(k - 6))
+            if s == 0 and is_quad(q - 2):
+                add_bias(vector_tile(q - 2))
+            if is_slot(k):
+                project_and_park(tensor_tile(k), k)
+            if is_slot(k - 1):
+                fetch_heads(tensor_tile(k - 1), k - 1)
+            if s == 0 and is_quad(q):
+                vector_project(q, 0)
+            if s == 1 and is_quad(q + 1):
+                vector_project(q + 1, 1)
+            if is_slot(k - 4):
+                normalise(tensor_tile(k - 4), 1)
+            if is_slot(k - 5):
+                quantise_r(tensor_tile(k - 5))
+            if s == 2 and is_quad(q - 1):
+                quantise_r(vector_tile(q - 1))
+            if is_slot(k - 3):
+                mix_on_tensor(tensor_tile(k - 3))
+            if is_slot(k):
+                build_blocks(tensor_tile(k))
+            if s == 0 and is_quad(q - 1):
+                vector_measure(q - 1)
+            if s == 1 and is_quad(q + 1):
+                vector_products(q + 1, H - 2)
+            if s == 2 and is_quad(q + 1):
+                vector_products(q + 1, H - 1)
+            if is_quad(q):
+                vector_add_heads(q, ((4, 5), (0, 1), (2, 3))[s])
+            if is_slot(k - 3):
+                measure(tensor_tile(k - 3), 0)
+                normalise(tensor_tile(k - 3), 0)
+                measure(tensor_tile(k - 3), 1)
+            if s == 0 and is_quad(q - 1):
+                vector_normalise(q - 1)
+            if is_slot(k - 4):
+                transpose_r(tensor_tile(k - 4))
+            if s == 1 and is_quad(q - 1):
+                transpose_r(vector_tile(q - 1))
+            if s < QUAD // PAIR and is_quad(q + 2):
+                transpose_x(q + 2, s)
+            if s == 2 and is_quad(q + 2):
+                quantise_x(q + 2)
+            if is_slot(k - 5):
+                project_out(tensor_tile(k - 5))
+            if s == 2 and is_quad(q - 1):
+                project_out(vector_tile(q - 1))
+            if s == 2 and is_quad(q + 1):
+                vector_join(q + 1)
+            if is_slot(k - 7):
+                store_out(tensor_tile(k - 7), k)
+            if s == 1 and is_quad(q - 2):
+                store_out(vector_tile(q - 2), k)
+            if s == 0 and is_quad(q + 3):
+                load_x(q + 3)
+
+        FIRST_SLOT = -3 * TENSOR_TILES
+        DIFF_SLOT = -TENSOR_TILES
+        WO_SLOT = 1
+        for k in range(FIRST_SLOT, N_SLOTS + 8):
+            if k == FIRST_SLOT + 1:
+                load_diff()
+                prepare_wv()
+            if k == FIRST_SLOT + TENSOR_TILES + 1:
+                load_wo()
+            if k == DIFF_SLOT:
+                prepare_diff()
+            if k == WO_SLOT:
+                prepare_wo()
+            slot(k)

@@ -11,7 +11,6 @@ U8 = mybir.dt.uint8
 FP8X4 = mybir.dt.float8_e4m3fn_x4
 ACT = mybir.ActivationFunctionType
 ALU = mybir.AluOpType
-AXIS = mybir.AxisListType
 
 P = 128
 PACK = 4
@@ -30,6 +29,7 @@ N_SLOTS = N_QUADS * TENSOR_TILES
 PAIR = 2
 GROUP = P // H
 GROUPS = P // GROUP
+BLOCK_TILES = 2
 PARKING_SLOTS = 4
 FIRST_PARKED = N_TILES - 2 * PARKING_SLOTS
 L0 = 0.8 - 0.6 * math.exp(-0.3 * 12)
@@ -77,10 +77,10 @@ def tile_differentialattention_pb_t_kernel(tc, x, diff, Wv, Wo, bo, out):
         nc.vector.tensor_scalar(
             out=eps_term[:], in0=ident_f32[:, 0:1], scalar1=0.0, scalar2=EPS / (GAIN * GAIN), op0=ALU.mult, op1=ALU.add
         )
-        same_token = keep.tile([P, GROUP], F32)
-        nc.vector.tensor_reduce(
-            out=same_token[:], in_=ident_f32[:].rearrange("p (t h) -> p t h", h=H), axis=AXIS.X, op=ALU.add
-        )
+        block_tiles = []
+        for n in range(BLOCK_TILES):
+            block_tiles.append(keep.tile([P, TENSOR_TILES * GROUPS, GROUP, H], F32, name="blocks%d" % n))
+            nc.gpsimd.memset(block_tiles[n][:], 0.0)
 
         wv_codes = keep.tile([P, DIM], U32, align_bytes=64)
         wv_scales = keep.tile([P, DIM], U8, align_bytes=64)
@@ -91,7 +91,7 @@ def tile_differentialattention_pb_t_kernel(tc, x, diff, Wv, Wo, bo, out):
         bias = keep.tile([P, C], F32)
 
         def prepare_wv():
-            grouped = keep.tile([P, DIM * PACK], BF16, align_bytes=64, name="wv_grouped")
+            grouped = keep.tile([P, DIM * PACK], BF16, align_bytes=64, name="wv_grouped", tag="w_grouped")
             grouped_words = grouped[:].bitcast(F32).rearrange("p (s w u) -> p s w u", w=P, u=2)
             for pair in range(DIM // P // PAIR):
                 wv_t = psum.tile([P, PAIR, 2, P], F32, tag="misc")
@@ -119,7 +119,7 @@ def tile_differentialattention_pb_t_kernel(tc, x, diff, Wv, Wo, bo, out):
                 nc.scalar.copy(out=head_weight[:, y * P : (y + 1) * P, :], in_=diff_t[:].rearrange("p a g -> p g a"))
 
         def prepare_wo():
-            grouped = keep.tile([P, 2, C, PACK], BF16, align_bytes=64, name="wo_grouped")
+            grouped = keep.tile([P, 2, C, PACK], BF16, align_bytes=64, name="wo_grouped", tag="w_grouped")
             for r in range(C // P):
                 wo_t = psum.tile([P, H, P], BF16, tag="misc")
                 for a in range(H):
@@ -136,7 +136,6 @@ def tile_differentialattention_pb_t_kernel(tc, x, diff, Wv, Wo, bo, out):
         x_grouped = {}
         x_codes = {}
         v_heads = {}
-        blocks = {}
         mix_banks = {}
         rms = {}
         vector_v = {}
@@ -208,7 +207,7 @@ def tile_differentialattention_pb_t_kernel(tc, x, diff, Wv, Wo, bo, out):
             return out_rows[first_row : first_row + 2 * P, :].rearrange("r c -> (r c)")
 
         def project_and_park(i, k):
-            v_sb = stage.tile([P, DIM], F32, name="v_sb")
+            v_sb = stage.tile([P, DIM], F32, name="v_sb", bufs=2)
             for bank in range(DIM // BANK):
                 v_bank = psum.tile([P, BANK], F32, tag="misc")
                 project_v(i, bank, v_bank[:])
@@ -219,14 +218,14 @@ def tile_differentialattention_pb_t_kernel(tc, x, diff, Wv, Wo, bo, out):
             v_heads[i] = stage.tile([P, GROUPS, HD], F32, name="v_heads", bufs=5)
             nc.sync.dma_start(out=v_heads[i][:], in_=parking_space(k).rearrange("(g p d) -> p g d", g=GROUPS, p=P))
 
-        def build_blocks(i):
-            blocks[i] = stage.tile([P, GROUPS, GROUP, H], F32, name="blocks", bufs=5)
-            nc.gpsimd.tensor_tensor(
-                out=blocks[i][:],
-                in0=head_weight[:, i * GROUPS : (i + 1) * GROUPS, :].unsqueeze(2).to_broadcast([P, GROUPS, GROUP, H]),
-                in1=same_token[:].unsqueeze(1).unsqueeze(3).to_broadcast([P, GROUPS, GROUP, H]),
-                op=ALU.mult,
-            )
+        def build_blocks(q):
+            blocks = block_tiles[q % BLOCK_TILES]
+            first = q * QUAD * GROUPS
+            for t in range(GROUP):
+                rows = slice(t * H, (t + 1) * H)
+                nc.sync.dma_start(
+                    out=blocks[rows, :, t, :], in_=head_weight[rows, first : first + TENSOR_TILES * GROUPS, :]
+                )
 
         def mix_on_tensor(i):
             for bank in range(GROUPS // HEADS_PER_BANK):
@@ -235,7 +234,7 @@ def tile_differentialattention_pb_t_kernel(tc, x, diff, Wv, Wo, bo, out):
                     g = bank * HEADS_PER_BANK + s
                     nc.tensor.matmul(
                         out=mix_banks[(i, bank)][:, s, :],
-                        lhsT=blocks[i][:, g].rearrange("p t a -> p (t a)"),
+                        lhsT=block_tiles[(i // QUAD) % BLOCK_TILES][:, (i % QUAD) * GROUPS + g].rearrange("p t a -> p (t a)"),
                         rhs=v_heads[i][:, g, :],
                         start=True,
                         stop=True,
@@ -278,7 +277,7 @@ def tile_differentialattention_pb_t_kernel(tc, x, diff, Wv, Wo, bo, out):
                 )
 
         def vector_join(q):
-            vector_mix[q] = stage.tile([P, H, HD], F32, name="vector_mix")
+            vector_mix[q] = stage.tile([P, H, HD], F32, name="vector_mix", bufs=2)
             nc.gpsimd.tensor_tensor(out=vector_mix[q][:], in0=products[q][:, 0], in1=products[q][:, 1], op=ALU.add)
 
         def vector_add_heads(q, heads):
@@ -305,25 +304,27 @@ def tile_differentialattention_pb_t_kernel(tc, x, diff, Wv, Wo, bo, out):
                 by_pass = r_t[:].rearrange("p (q j t) -> p q t j", q=2, j=PACK)
             else:
                 by_pass = r_t[:].rearrange("p (t q j) -> p q t j", q=2, j=PACK)
-            r_grouped[i] = stage.tile([P, 2, P, PACK], BF16, align_bytes=64, name="r_grouped")
-            nc.scalar.copy(out=r_grouped[i][:], in_=by_pass)
+            if i // QUAD not in r_grouped:
+                r_grouped[i // QUAD] = stage.tile([P, QUAD, 2, P, PACK], BF16, align_bytes=64, name="r_grouped", bufs=2)
+            nc.scalar.copy(out=r_grouped[i // QUAD][:, i % QUAD], in_=by_pass)
 
-        def quantise_r(i):
-            codes = stage.tile([P, 2 * P], U32, align_bytes=64, name="r_codes")
-            scales = stage.tile([P, 2 * P], U8, align_bytes=64, name="r_scales")
+        def quantise_r(q):
+            codes = stage.tile([P, QUAD * 2 * P], U32, align_bytes=64, name="r_codes", bufs=2)
+            scales = stage.tile([P, QUAD * 2 * P], U8, align_bytes=64, name="r_scales", bufs=2)
             nc.vector.quantize_mx(
-                out=codes[:].bitcast(FP8X4), scales=scales[:], in_=r_grouped[i][:].rearrange("p q t j -> p (q t j)")
+                out=codes[:].bitcast(FP8X4), scales=scales[:], in_=r_grouped[q][:].rearrange("p s q t j -> p (s q t j)")
             )
-            r_codes[i] = (codes, scales)
+            r_codes[q] = (codes, scales)
 
         def project_out(i):
-            codes, scales = r_codes[i]
+            codes, scales = r_codes[i // QUAD]
             acc[i] = psum.tile([P, C], F32, tag="misc", name="acc")
             for g in range(2):
+                tok = slice(((i % QUAD) * 2 + g) * P, ((i % QUAD) * 2 + g + 1) * P)
                 nc.tensor.matmul_mx(
                     out=acc[i][:],
-                    lhsT=codes[:, g * P : (g + 1) * P].bitcast(FP8X4),
-                    lhsT_scale=scales[:, g * P : (g + 1) * P],
+                    lhsT=codes[:, tok].bitcast(FP8X4),
+                    lhsT_scale=scales[:, tok],
                     rhs=wo_codes[:, g * C : (g + 1) * C].bitcast(FP8X4),
                     rhs_scale=wo_scales[:, g * C : (g + 1) * C],
                     start=(g == 0),
@@ -331,9 +332,9 @@ def tile_differentialattention_pb_t_kernel(tc, x, diff, Wv, Wo, bo, out):
                 )
 
         def add_bias(i):
-            product = stage.tile([P, C], F32, name="product", bufs=4)
+            product = stage.tile([P, C], F32, name="product")
             nc.scalar.copy(out=product[:], in_=acc[i][:])
-            out_sb[i] = stage.tile([P, C], F32, name="out_sb", bufs=6)
+            out_sb[i] = stage.tile([P, C], F32, name="out_sb", bufs=4)
             nc.gpsimd.tensor_tensor(out=out_sb[i][:], in0=product[:], in1=bias[:], op=ALU.add)
 
         def store_out(i, k):
@@ -351,9 +352,9 @@ def tile_differentialattention_pb_t_kernel(tc, x, diff, Wv, Wo, bo, out):
 
         def slot(k):
             q, s = divmod(k, TENSOR_TILES)
-            if is_slot(k - 6):
-                add_bias(tensor_tile(k - 6))
-            if s == 0 and is_quad(q - 2):
+            if is_slot(k - 8):
+                add_bias(tensor_tile(k - 8))
+            if s == 2 and is_quad(q - 2):
                 add_bias(vector_tile(q - 2))
             if is_slot(k):
                 project_and_park(tensor_tile(k), k)
@@ -365,14 +366,12 @@ def tile_differentialattention_pb_t_kernel(tc, x, diff, Wv, Wo, bo, out):
                 vector_project(q + 1, 1)
             if is_slot(k - 4):
                 normalise(tensor_tile(k - 4), 1)
-            if is_slot(k - 5):
-                quantise_r(tensor_tile(k - 5))
-            if s == 2 and is_quad(q - 1):
-                quantise_r(vector_tile(q - 1))
+            if s == 1 and is_quad(q - 2):
+                quantise_r(q - 2)
             if is_slot(k - 3):
                 mix_on_tensor(tensor_tile(k - 3))
-            if is_slot(k):
-                build_blocks(tensor_tile(k))
+            if s == 0 and is_quad(q):
+                build_blocks(q)
             if s == 0 and is_quad(q - 1):
                 vector_measure(q - 1)
             if s == 1 and is_quad(q + 1):
@@ -395,23 +394,23 @@ def tile_differentialattention_pb_t_kernel(tc, x, diff, Wv, Wo, bo, out):
                 transpose_x(q + 2, s)
             if s == 2 and is_quad(q + 2):
                 quantise_x(q + 2)
-            if is_slot(k - 5):
-                project_out(tensor_tile(k - 5))
-            if s == 2 and is_quad(q - 1):
-                project_out(vector_tile(q - 1))
+            if is_slot(k - 7):
+                project_out(tensor_tile(k - 7))
+            if s == 1 and is_quad(q - 2):
+                project_out(vector_tile(q - 2))
             if s == 2 and is_quad(q + 1):
                 vector_join(q + 1)
-            if is_slot(k - 7):
-                store_out(tensor_tile(k - 7), k)
-            if s == 1 and is_quad(q - 2):
-                store_out(vector_tile(q - 2), k)
+            if is_slot(k - 9):
+                store_out(tensor_tile(k - 9), k)
+            if s == 0 and is_quad(q - 3):
+                store_out(vector_tile(q - 3), k)
             if s == 0 and is_quad(q + 3):
                 load_x(q + 3)
 
         FIRST_SLOT = -3 * TENSOR_TILES
         DIFF_SLOT = -TENSOR_TILES
         WO_SLOT = 1
-        for k in range(FIRST_SLOT, N_SLOTS + 8):
+        for k in range(FIRST_SLOT, N_SLOTS + 10):
             if k == FIRST_SLOT + 1:
                 load_diff()
                 prepare_wv()

@@ -186,20 +186,15 @@ def tile_differentialattention_pb_t_kernel(tc, x, diff, Wv, Wo, bo, out):
                 stop=True,
             )
 
-        def root_mean_square(values, count):
+        def inverse_rms(values, count):
             sumsq = stage.tile([P, count], F32, name="sumsq")
             for s in range(count):
                 square = stage.tile([P, HD], BF16, name="square")
                 nc.scalar.activation(out=square[:], in_=values[:, s, :], func=ACT.Square, accum_out=sumsq[:, s : s + 1])
-            root = stage.tile([P, count], F32, name="root", bufs=4)
-            nc.scalar.activation(
-                out=root[:], in_=sumsq[:], func=ACT.Sqrt, scale=1.0 / (HD * GAIN * GAIN), bias=eps_term[:]
-            )
-            return root
-
-        def reciprocal(root, count):
             inv = stage.tile([P, count], F32, name="inv", bufs=6)
-            nc.vector.reciprocal(out=inv[:], in_=root[:])
+            nc.scalar.activation(
+                out=inv[:], in_=sumsq[:], func=ACT.Abs_reciprocal_sqrt, scale=1.0 / (HD * GAIN * GAIN), bias=eps_term[:]
+            )
             return inv[:].unsqueeze(2).to_broadcast([P, count, HD])
 
         def parking_space(k):
@@ -241,7 +236,7 @@ def tile_differentialattention_pb_t_kernel(tc, x, diff, Wv, Wo, bo, out):
                     )
 
         def measure(i, bank):
-            rms[(i, bank)] = root_mean_square(mix_banks[(i, bank)], HEADS_PER_BANK)
+            rms[(i, bank)] = inverse_rms(mix_banks[(i, bank)], HEADS_PER_BANK)
 
         def normalise(i, bank):
             if bank == 0:
@@ -249,7 +244,7 @@ def tile_differentialattention_pb_t_kernel(tc, x, diff, Wv, Wo, bo, out):
             nc.vector.tensor_tensor(
                 out=r[i][:, bank * HEADS_PER_BANK : (bank + 1) * HEADS_PER_BANK, :],
                 in0=mix_banks[(i, bank)][:],
-                in1=reciprocal(rms[(i, bank)], HEADS_PER_BANK),
+                in1=rms[(i, bank)],
                 op=ALU.mult,
             )
 
@@ -289,12 +284,12 @@ def tile_differentialattention_pb_t_kernel(tc, x, diff, Wv, Wo, bo, out):
                     )
 
         def vector_measure(q):
-            rms[vector_tile(q)] = root_mean_square(vector_mix[q], H)
+            rms[vector_tile(q)] = inverse_rms(vector_mix[q], H)
 
         def vector_normalise(q):
             i = vector_tile(q)
             r[i] = stage.tile([P, H, HD], BF16, name="r", bufs=4)
-            nc.gpsimd.tensor_tensor(out=r[i][:], in0=vector_mix[q][:], in1=reciprocal(rms[i], H), op=ALU.mult)
+            nc.gpsimd.tensor_tensor(out=r[i][:], in0=vector_mix[q][:], in1=rms[i], op=ALU.mult)
 
         def transpose_r(i):
             r_t = psum.tile([P, H * P], BF16, tag="misc")

@@ -24,11 +24,13 @@ HEADS_PER_BANK = BANK // HD
 N_TILES = TOKENS // P
 QUAD = 4
 N_QUADS = N_TILES // QUAD
+N_VECTOR = N_QUADS - 1
+N_TENSOR = N_TILES - N_VECTOR
 TENSOR_TILES = QUAD - 1
-N_SLOTS = N_QUADS * TENSOR_TILES
 PAIR = 2
 GROUP = P // H
 GROUPS = P // GROUP
+CLUSTER = 4
 BLOCK_TILES = 2
 PARKING_SLOTS = 4
 FIRST_PARKED = N_TILES - 2 * PARKING_SLOTS
@@ -52,35 +54,52 @@ def tile_differentialattention_pb_t_kernel(tc, x, diff, Wv, Wo, bo, out):
         stack.enter_context(tc.manual_schedule())
 
         wv_raw = keep.tile([P, DIM // P, C], BF16)
-        nc.sync.dma_start(out=wv_raw[:], in_=Wv.rearrange("(r p) k -> p r k", p=P))
         vector_diff_raw = keep.tile([P, N_QUADS, H * H], BF16)
         diff_groups = keep.tile([P, 2, GROUP * H * H], BF16)
         wo_raw = keep.tile([P, C // P, DIM], BF16)
         bias_raw = keep.tile([P, C], BF16)
 
-        def load_diff():
+        def load_wv(half):
+            rows = slice(half * DIM // 2, (half + 1) * DIM // 2)
+            tiles = slice(half * DIM // P // 2, (half + 1) * DIM // P // 2)
+            nc.sync.dma_start(out=wv_raw[:, tiles, :], in_=Wv[rows, :].rearrange("(r p) k -> p r k", p=P))
+
+        def load_vector_diff():
             nc.sync.dma_start(
                 out=vector_diff_raw[:],
                 in_=diff_rows.rearrange("(q s p) c -> p q s c", s=QUAD, p=P)[:, :, QUAD - 1, :],
             )
-            nc.sync.dma_start(out=diff_groups[:], in_=diff_rows.rearrange("(y g t) c -> g y (t c)", y=2, t=GROUP))
+
+        def load_diff_groups(y):
+            rows = slice(y * TOKENS // 2, (y + 1) * TOKENS // 2)
+            nc.sync.dma_start(out=diff_groups[:, y, :], in_=diff_rows[rows, :].rearrange("(g t) c -> g (t c)", t=GROUP))
 
         def load_wo():
             nc.sync.dma_start(out=wo_raw[:], in_=Wo.rearrange("(r p) k -> p r k", p=P))
             nc.sync.dma_start(out=bias_raw[:], in_=bo.partition_broadcast(P))
 
         ident_f32 = keep.tile([P, P], F32)
-        make_identity(nc, ident_f32[:])
         ident_bf16 = keep.tile([P, P], BF16)
-        make_identity(nc, ident_bf16[:])
+        of_place = keep.tile([P, CLUSTER], F32)
         eps_term = keep.tile([P, 1], F32)
-        nc.vector.tensor_scalar(
-            out=eps_term[:], in0=ident_f32[:, 0:1], scalar1=0.0, scalar2=EPS / (GAIN * GAIN), op0=ALU.mult, op1=ALU.add
-        )
         block_tiles = []
         for n in range(BLOCK_TILES):
-            block_tiles.append(keep.tile([P, TENSOR_TILES * GROUPS, GROUP, H], F32, name="blocks%d" % n))
-            nc.gpsimd.memset(block_tiles[n][:], 0.0)
+            block_tiles.append(keep.tile([P, QUAD * GROUPS, GROUP, H], F32, name="blocks%d" % n))
+
+        def make_constants():
+            make_identity(nc, ident_f32[:])
+            make_identity(nc, ident_bf16[:])
+            nc.vector.tensor_scalar(
+                out=eps_term[:], in0=ident_f32[:, 0:1], scalar1=0.0, scalar2=EPS / (GAIN * GAIN), op0=ALU.mult, op1=ALU.add
+            )
+            nc.vector.tensor_reduce(
+                out=of_place[:],
+                in_=ident_f32[:].rearrange("p (c j h) -> p j c h", j=CLUSTER, h=H),
+                op=ALU.add,
+                axis=mybir.AxisListType.XY,
+            )
+            for n in range(BLOCK_TILES):
+                nc.gpsimd.memset(block_tiles[n][:], 0.0)
 
         wv_codes = keep.tile([P, DIM], U32, align_bytes=64)
         wv_scales = keep.tile([P, DIM], U8, align_bytes=64)
@@ -89,46 +108,59 @@ def tile_differentialattention_pb_t_kernel(tc, x, diff, Wv, Wo, bo, out):
         vector_diff = keep.tile([P, N_QUADS, H * H], F32)
         head_weight = keep.tile([P, 2 * P, H], F32)
         bias = keep.tile([P, C], F32)
+        wv_grouped = keep.tile([P, DIM * PACK], BF16, align_bytes=64, name="wv_grouped", tag="w_grouped")
 
-        def prepare_wv():
-            grouped = keep.tile([P, DIM * PACK], BF16, align_bytes=64, name="wv_grouped", tag="w_grouped")
-            grouped_words = grouped[:].bitcast(F32).rearrange("p (s w u) -> p s w u", w=P, u=2)
-            for pair in range(DIM // P // PAIR):
-                wv_t = psum.tile([P, PAIR, 2, P], F32, tag="misc")
-                for s in range(PAIR):
-                    words = wv_raw[:, pair * PAIR + s, :].bitcast(F32)
-                    for u in range(2):
-                        nc.tensor.transpose(wv_t[:, s, u, :], words[:, u * P : (u + 1) * P], ident_f32[:])
-                nc.vector.tensor_copy(
-                    out=grouped_words[:, pair * PAIR : (pair + 1) * PAIR], in_=wv_t[:].rearrange("p s u w -> p s w u")
-                )
-            nc.vector.quantize_mx(out=wv_codes[:].bitcast(FP8X4), scales=wv_scales[:], in_=grouped[:])
+        def transpose_wv(pair):
+            grouped_words = wv_grouped[:].bitcast(F32).rearrange("p (s w u) -> p s w u", w=P, u=2)
+            wv_t = psum.tile([P, PAIR, 2, P], F32, tag="mix")
+            for s in range(PAIR):
+                words = wv_raw[:, pair * PAIR + s, :].bitcast(F32)
+                for u in range(2):
+                    nc.tensor.transpose(wv_t[:, s, u, :], words[:, u * P : (u + 1) * P], ident_f32[:])
+            out_words = grouped_words[:, pair * PAIR : (pair + 1) * PAIR]
+            in_words = wv_t[:].rearrange("p s u w -> p s w u")
+            if pair % 2 == 0:
+                nc.vector.tensor_copy(out=out_words, in_=in_words)
+            else:
+                nc.scalar.copy(out=out_words, in_=in_words)
 
-        def prepare_diff():
-            nc.vector.tensor_copy(out=vector_diff[:], in_=vector_diff_raw[:])
-            diff_by_a = keep.tile([P, 2, H, GROUP, H], BF16)
-            for y in range(2):
-                nc.vector.tensor_copy(
-                    out=diff_by_a[:, y], in_=diff_groups[:, y, :].rearrange("p (t a h) -> p a t h", a=H, h=H)
-                )
-                diff_t = psum.tile([P, H, P], BF16, tag="misc")
-                for a in range(H):
-                    nc.tensor.transpose(
-                        diff_t[:, a, :], diff_by_a[:, y, a].rearrange("p t h -> p (t h)"), ident_bf16[:]
-                    )
-                nc.scalar.copy(out=head_weight[:, y * P : (y + 1) * P, :], in_=diff_t[:].rearrange("p a g -> p g a"))
-
-        def prepare_wo():
-            grouped = keep.tile([P, 2, C, PACK], BF16, align_bytes=64, name="wo_grouped", tag="w_grouped")
-            for r in range(C // P):
-                wo_t = psum.tile([P, H, P], BF16, tag="misc")
-                for a in range(H):
-                    nc.tensor.transpose(wo_t[:, a, :], wo_raw[:, r, a * HD : (a + 1) * HD], ident_bf16[:])
-                nc.scalar.copy(
-                    out=grouped[:, :, r * P : (r + 1) * P, :], in_=wo_t[:].rearrange("p (g j) c -> p g c j", j=PACK)
-                )
+        def quantise_wv(half):
+            cols = slice(half * DIM // 2, (half + 1) * DIM // 2)
+            vals = slice(half * DIM * PACK // 2, (half + 1) * DIM * PACK // 2)
             nc.vector.quantize_mx(
-                out=wo_codes[:].bitcast(FP8X4), scales=wo_scales[:], in_=grouped[:].rearrange("p g c j -> p (g c j)")
+                out=wv_codes[:, cols].bitcast(FP8X4), scales=wv_scales[:, cols], in_=wv_grouped[:, vals]
+            )
+
+        diff_by_a = keep.tile([P, 2, H, GROUP, H], BF16)
+
+        def sort_diff(y):
+            nc.vector.tensor_copy(
+                out=diff_by_a[:, y], in_=diff_groups[:, y, :].rearrange("p (t a h) -> p a t h", a=H, h=H)
+            )
+
+        def turn_diff(y):
+            diff_t = psum.tile([P, H, P], BF16, tag="misc")
+            for a in range(H):
+                nc.tensor.transpose(
+                    diff_t[:, a, :], diff_by_a[:, y, a].rearrange("p t h -> p (t h)"), ident_bf16[:]
+                )
+            nc.scalar.copy(out=head_weight[:, y * P : (y + 1) * P, :], in_=diff_t[:].rearrange("p a g -> p g a"))
+
+        wo_grouped = []
+
+        def transpose_wo(r):
+            if r == 0:
+                wo_grouped.append(keep.tile([P, 2, C, PACK], BF16, align_bytes=64, name="wo_grouped", tag="w_grouped"))
+            wo_t = psum.tile([P, H, P], BF16, tag="misc")
+            for a in range(H):
+                nc.tensor.transpose(wo_t[:, a, :], wo_raw[:, r, a * HD : (a + 1) * HD], ident_bf16[:])
+            nc.scalar.copy(
+                out=wo_grouped[0][:, :, r * P : (r + 1) * P, :], in_=wo_t[:].rearrange("p (g j) c -> p g c j", j=PACK)
+            )
+
+        def quantise_wo():
+            nc.vector.quantize_mx(
+                out=wo_codes[:].bitcast(FP8X4), scales=wo_scales[:], in_=wo_grouped[0][:].rearrange("p g c j -> p (g c j)")
             )
             nc.vector.tensor_copy(out=bias[:], in_=bias_raw[:])
 
@@ -141,11 +173,19 @@ def tile_differentialattention_pb_t_kernel(tc, x, diff, Wv, Wo, bo, out):
         vector_v = {}
         products = {}
         vector_mix = {}
+        vector_sumsq = {}
         r = {}
         r_grouped = {}
         r_codes = {}
         acc = {}
         out_sb = {}
+        stored = set()
+        built = {}
+        normalised = set()
+        mixed = set()
+
+        def is_vector(i):
+            return i % QUAD == QUAD - 1 and i // QUAD < N_VECTOR
 
         def load_x(q):
             x_raw[q] = stage.tile([P, QUAD, C], BF16, name="x_raw")
@@ -154,7 +194,7 @@ def tile_differentialattention_pb_t_kernel(tc, x, diff, Wv, Wo, bo, out):
             )
 
         def transpose_x(q, pair):
-            if pair == 0:
+            if q not in x_grouped:
                 x_grouped[q] = stage.tile([P, QUAD * P * PACK], BF16, align_bytes=64, name="x_grouped", bufs=2)
             grouped_words = x_grouped[q][:].bitcast(F32).rearrange("p (s t u) -> p s t u", t=P, u=2)
             x_t = psum.tile([P, PAIR, 2, P], F32, tag="misc")
@@ -162,9 +202,8 @@ def tile_differentialattention_pb_t_kernel(tc, x, diff, Wv, Wo, bo, out):
                 words = x_raw[q][:, pair * PAIR + s, :].bitcast(F32)
                 for u in range(2):
                     nc.tensor.transpose(x_t[:, s, u, :], words[:, u * P : (u + 1) * P], ident_f32[:])
-            nc.scalar.copy(
-                out=grouped_words[:, pair * PAIR : (pair + 1) * PAIR], in_=x_t[:].rearrange("p s u t -> p s t u")
-            )
+            copy = nc.vector.tensor_copy if (q, pair) == (0, 1) else nc.scalar.copy
+            copy(out=grouped_words[:, pair * PAIR : (pair + 1) * PAIR], in_=x_t[:].rearrange("p s u t -> p s t u"))
 
         def quantise_x(q):
             codes = stage.tile([P, QUAD * P], U32, align_bytes=64, name="x_codes")
@@ -186,59 +225,102 @@ def tile_differentialattention_pb_t_kernel(tc, x, diff, Wv, Wo, bo, out):
                 stop=True,
             )
 
-        def inverse_rms(values, count):
-            sumsq = stage.tile([P, count], F32, name="sumsq")
-            for s in range(count):
+        def squares_of(values, sumsq, runs):
+            for s in runs:
                 square = stage.tile([P, HD], BF16, name="square")
                 nc.scalar.activation(out=square[:], in_=values[:, s, :], func=ACT.Square, accum_out=sumsq[:, s : s + 1])
+
+        def inverse_rms(sumsq, count):
             inv = stage.tile([P, count], F32, name="inv", bufs=6)
             nc.scalar.activation(
                 out=inv[:], in_=sumsq[:], func=ACT.Abs_reciprocal_sqrt, scale=1.0 / (HD * GAIN * GAIN), bias=eps_term[:]
             )
             return inv[:].unsqueeze(2).to_broadcast([P, count, HD])
 
+        def tensor_tile(k):
+            q = min(k // TENSOR_TILES, N_QUADS - 1)
+            return q * QUAD + k - q * TENSOR_TILES
+
+        def parking_pair(k):
+            pair = k % PARKING_SLOTS
+            return pair if k < N_TENSOR - PARKING_SLOTS else PARKING_SLOTS - 2 + k % 2
+
         def parking_space(k):
-            first_row = (FIRST_PARKED + 2 * (k % PARKING_SLOTS)) * P
+            first_row = (FIRST_PARKED + 2 * parking_pair(k)) * P
             return out_rows[first_row : first_row + 2 * P, :].rearrange("r c -> (r c)")
 
-        def project_and_park(i, k):
-            v_sb = stage.tile([P, DIM], F32, name="v_sb", bufs=2)
+        def project_and_park(k):
+            i = tensor_tile(k)
+            assert not any(FIRST_PARKED + 2 * parking_pair(k) + n in stored for n in range(2))
+            v_sb = stage.tile([P, DIM], F32, name="v_sb", bufs=3)
             for bank in range(DIM // BANK):
                 v_bank = psum.tile([P, BANK], F32, tag="misc")
                 project_v(i, bank, v_bank[:])
-                nc.vector.tensor_copy(out=v_sb[:, bank * BANK : (bank + 1) * BANK], in_=v_bank[:])
+                v_half = v_sb[:, bank * BANK : (bank + 1) * BANK]
+                if bank == 1 and (k < MIX_LAG or False):
+                    nc.scalar.copy(out=v_half, in_=v_bank[:])
+                else:
+                    nc.vector.tensor_copy(out=v_half, in_=v_bank[:])
             nc.sync.dma_start(out=parking_space(k).rearrange("(t w) -> t w", t=P), in_=v_sb[:])
 
-        def fetch_heads(i, k):
+        def fetch_heads(k):
+            i = tensor_tile(k)
             v_heads[i] = stage.tile([P, GROUPS, HD], F32, name="v_heads", bufs=5)
             nc.sync.dma_start(out=v_heads[i][:], in_=parking_space(k).rearrange("(g p d) -> p g d", g=GROUPS, p=P))
 
-        def build_blocks(q):
-            blocks = block_tiles[q % BLOCK_TILES]
+        def quad_groups(q):
+            return (TENSOR_TILES if q < N_VECTOR else QUAD) * GROUPS
+
+        def build_blocks(q, tokens):
             first = q * QUAD * GROUPS
-            for t in range(GROUP):
+            built.setdefault(q, []).extend(tokens)
+            assert q < 2 or ((q - 2) * TENSOR_TILES + 2, 1) in mixed
+            for t in tokens:
                 rows = slice(t * H, (t + 1) * H)
                 nc.sync.dma_start(
-                    out=blocks[rows, :, t, :], in_=head_weight[rows, first : first + TENSOR_TILES * GROUPS, :]
+                    out=block_tiles[q % BLOCK_TILES][rows, : quad_groups(q), t, :],
+                    in_=head_weight[rows, first : first + quad_groups(q), :],
                 )
 
-        def mix_on_tensor(i):
-            for bank in range(GROUPS // HEADS_PER_BANK):
-                mix_banks[(i, bank)] = psum.tile([P, HEADS_PER_BANK, HD], F32, tag="mix", name="mix_bank")
-                for s in range(HEADS_PER_BANK):
-                    g = bank * HEADS_PER_BANK + s
-                    nc.tensor.matmul(
-                        out=mix_banks[(i, bank)][:, s, :],
-                        lhsT=block_tiles[(i // QUAD) % BLOCK_TILES][:, (i % QUAD) * GROUPS + g].rearrange("p t a -> p (t a)"),
-                        rhs=v_heads[i][:, g, :],
-                        start=True,
-                        stop=True,
-                    )
+        def build_first_blocks():
+            squares = keep.tile([P, TENSOR_TILES * GROUPS, CLUSTER, H], F32)
+            for j in range(CLUSTER):
+                nc.gpsimd.tensor_scalar(
+                    out=squares[:, :, j, :], in0=head_weight[:, : TENSOR_TILES * GROUPS, :],
+                    scalar1=of_place[:, j : j + 1], scalar2=0.0, op0=ALU.mult, op1=ALU.add,
+                )
+            built[0] = list(range(GROUP))
+            for c in range(GROUP // CLUSTER):
+                rows = slice(c * CLUSTER * H, (c + 1) * CLUSTER * H)
+                nc.sync.dma_start(
+                    out=block_tiles[0][rows, : TENSOR_TILES * GROUPS, c * CLUSTER : (c + 1) * CLUSTER, :],
+                    in_=squares[rows],
+                )
 
-        def measure(i, bank):
-            rms[(i, bank)] = inverse_rms(mix_banks[(i, bank)], HEADS_PER_BANK)
+        def mix_on_tensor(k, bank):
+            i = tensor_tile(k)
+            mixed.add((k, bank))
+            assert len(built[i // QUAD]) == GROUP
+            mix_banks[(i, bank)] = psum.tile([P, HEADS_PER_BANK, HD], F32, tag="mix", name="mix_bank")
+            for s in range(HEADS_PER_BANK):
+                g = bank * HEADS_PER_BANK + s
+                nc.tensor.matmul(
+                    out=mix_banks[(i, bank)][:, s, :],
+                    lhsT=block_tiles[(i // QUAD) % BLOCK_TILES][:, (i % QUAD) * GROUPS + g].rearrange("p t a -> p (t a)"),
+                    rhs=v_heads[i][:, g, :],
+                    start=True,
+                    stop=True,
+                )
 
-        def normalise(i, bank):
+        def measure(k, bank):
+            i = tensor_tile(k)
+            sumsq = stage.tile([P, HEADS_PER_BANK], F32, name="sumsq")
+            squares_of(mix_banks[(i, bank)], sumsq, range(HEADS_PER_BANK))
+            rms[(i, bank)] = inverse_rms(sumsq, HEADS_PER_BANK)
+
+        def normalise(k, bank):
+            i = tensor_tile(k)
+            normalised.add((i, bank))
             if bank == 0:
                 r[i] = stage.tile([P, GROUPS, HD], BF16, name="r", bufs=4)
             nc.vector.tensor_tensor(
@@ -248,74 +330,78 @@ def tile_differentialattention_pb_t_kernel(tc, x, diff, Wv, Wo, bo, out):
                 op=ALU.mult,
             )
 
-        def vector_tile(q):
-            return q * QUAD + QUAD - 1
+        def vector_tile(w):
+            return w * QUAD + QUAD - 1
 
-        def vector_weight(q, a, h):
-            return vector_diff[:, q, a * H + h : a * H + h + 1]
+        def vector_weight(w, a, h):
+            return vector_diff[:, w, a * H + h : a * H + h + 1]
 
-        def vector_head(q, h):
+        def vector_head(w, h):
             col = (h % HEADS_PER_BANK) * HD
-            return vector_v[(q, h // HEADS_PER_BANK)][:, col : col + HD]
+            return vector_v[(w, h // HEADS_PER_BANK)][:, col : col + HD]
 
-        def vector_project(q, bank):
-            vector_v[(q, bank)] = psum.tile([P, BANK], F32, tag="vector_v%d" % bank, bufs=1, name="vector_v")
-            project_v(vector_tile(q), bank, vector_v[(q, bank)][:])
+        def vector_project(w, bank):
+            vector_v[(w, bank)] = psum.tile([P, BANK], F32, tag="vector_v%d" % bank, bufs=1, name="vector_v")
+            project_v(vector_tile(w), bank, vector_v[(w, bank)][:])
 
-        def vector_products(q, h):
-            if h == H - 2:
-                products[q] = stage.tile([P, 2, H, HD], F32, name="products", bufs=2)
-            for a in range(H):
+        def vector_products(w, h, sums):
+            if w == 0 and w not in vector_mix:
+                vector_mix[w] = stage.tile([P, H, HD], F32, name="vector_mix", bufs=2)
+            if w > 0 and w not in products:
+                products[w] = stage.tile([P, 2, H, HD], F32, name="products", bufs=2)
+            for a in sums:
                 nc.scalar.activation(
-                    out=products[q][:, h - (H - 2), a, :], in_=vector_head(q, h), func=ACT.Copy,
-                    scale=vector_weight(q, a, h),
+                    out=vector_mix[w][:, a, :] if w == 0 else products[w][:, h - (H - 2), a, :],
+                    in_=vector_head(w, h), func=ACT.Copy, scale=vector_weight(w, a, h),
                 )
 
-        def vector_join(q):
-            vector_mix[q] = stage.tile([P, H, HD], F32, name="vector_mix", bufs=2)
-            nc.gpsimd.tensor_tensor(out=vector_mix[q][:], in0=products[q][:, 0], in1=products[q][:, 1], op=ALU.add)
+        def vector_join(w):
+            vector_mix[w] = stage.tile([P, H, HD], F32, name="vector_mix", bufs=2)
+            nc.gpsimd.tensor_tensor(out=vector_mix[w][:], in0=products[w][:, 0], in1=products[w][:, 1], op=ALU.add)
 
-        def vector_add_heads(q, heads):
-            for h in heads:
-                for a in range(H):
-                    nc.vector.scalar_tensor_tensor(
-                        out=vector_mix[q][:, a, :], in0=vector_head(q, h), scalar=vector_weight(q, a, h),
-                        in1=vector_mix[q][:, a, :], op0=ALU.mult, op1=ALU.add,
-                    )
+        def vector_add_head(w, h, sums):
+            for a in sums:
+                nc.vector.scalar_tensor_tensor(
+                    out=vector_mix[w][:, a, :], in0=vector_head(w, h), scalar=vector_weight(w, a, h),
+                    in1=vector_mix[w][:, a, :], op0=ALU.mult, op1=ALU.add,
+                )
 
-        def vector_measure(q):
-            rms[vector_tile(q)] = inverse_rms(vector_mix[q], H)
+        def vector_measure(w, heads):
+            if w not in vector_sumsq:
+                vector_sumsq[w] = stage.tile([P, H], F32, name="vector_sumsq")
+            squares_of(vector_mix[w], vector_sumsq[w], heads)
 
-        def vector_normalise(q):
-            i = vector_tile(q)
+        def vector_normalise(w):
+            i = vector_tile(w)
+            rms[i] = inverse_rms(vector_sumsq[w], H)
             r[i] = stage.tile([P, H, HD], BF16, name="r", bufs=4)
-            nc.gpsimd.tensor_tensor(out=r[i][:], in0=vector_mix[q][:], in1=rms[i], op=ALU.mult)
+            nc.gpsimd.tensor_tensor(out=r[i][:], in0=vector_mix[w][:], in1=rms[i], op=ALU.mult)
 
         def transpose_r(i):
             r_t = psum.tile([P, H * P], BF16, tag="misc")
+            assert is_vector(i) or (i, 1) in normalised
             for s in range(H):
                 nc.tensor.transpose(r_t[:, s * P : (s + 1) * P], r[i][:, s, :], ident_bf16[:])
-            if i % QUAD == QUAD - 1:
+            if is_vector(i):
                 by_pass = r_t[:].rearrange("p (q j t) -> p q t j", q=2, j=PACK)
             else:
                 by_pass = r_t[:].rearrange("p (t q j) -> p q t j", q=2, j=PACK)
-            if i // QUAD not in r_grouped:
-                r_grouped[i // QUAD] = stage.tile([P, QUAD, 2, P, PACK], BF16, align_bytes=64, name="r_grouped", bufs=2)
-            nc.scalar.copy(out=r_grouped[i // QUAD][:, i % QUAD], in_=by_pass)
+            r_grouped[i] = stage.tile([P, 2, P, PACK], BF16, align_bytes=64, name="r_grouped", bufs=3)
+            nc.scalar.copy(out=r_grouped[i][:], in_=by_pass)
 
-        def quantise_r(q):
-            codes = stage.tile([P, QUAD * 2 * P], U32, align_bytes=64, name="r_codes", bufs=2)
-            scales = stage.tile([P, QUAD * 2 * P], U8, align_bytes=64, name="r_scales", bufs=2)
+        def quantise_r(i):
+            codes = stage.tile([P, 2 * P], U32, align_bytes=64, name="r_codes", bufs=3)
+            scales = stage.tile([P, 2 * P], U8, align_bytes=64, name="r_scales", bufs=3)
             nc.vector.quantize_mx(
-                out=codes[:].bitcast(FP8X4), scales=scales[:], in_=r_grouped[q][:].rearrange("p s q t j -> p (s q t j)")
+                out=codes[:].bitcast(FP8X4), scales=scales[:], in_=r_grouped[i][:].rearrange("p q t j -> p (q t j)")
             )
-            r_codes[q] = (codes, scales)
+            r_codes[i] = (codes, scales)
 
         def project_out(i):
-            codes, scales = r_codes[i // QUAD]
+            codes, scales = r_codes[i]
             acc[i] = psum.tile([P, C], F32, tag="misc", name="acc")
             for g in range(2):
-                tok = slice(((i % QUAD) * 2 + g) * P, ((i % QUAD) * 2 + g + 1) * P)
+                tok = slice(g * P, (g + 1) * P)
                 nc.tensor.matmul_mx(
                     out=acc[i][:],
                     lhsT=codes[:, tok].bitcast(FP8X4),
@@ -327,92 +413,195 @@ def tile_differentialattention_pb_t_kernel(tc, x, diff, Wv, Wo, bo, out):
                 )
 
         def add_bias(i):
+            if i >= N_TILES - 2:
+                out_sb[i] = stage.tile([P, C], F32, name="out_sb", bufs=4)
+                nc.vector.tensor_tensor(out=out_sb[i][:], in0=acc[i][:], in1=bias[:], op=ALU.add)
+                return
             product = stage.tile([P, C], F32, name="product")
             nc.scalar.copy(out=product[:], in_=acc[i][:])
             out_sb[i] = stage.tile([P, C], F32, name="out_sb", bufs=4)
             nc.gpsimd.tensor_tensor(out=out_sb[i][:], in0=product[:], in1=bias[:], op=ALU.add)
 
-        def store_out(i, k):
-            assert i < FIRST_PARKED or k > N_SLOTS - PARKING_SLOTS + (i - FIRST_PARKED) // 2 + 1
+        def store_out(i):
+            stored.add(i)
             nc.sync.dma_start(out=out_rows[i * P : (i + 1) * P, :], in_=out_sb[i][:])
 
-        def tensor_tile(k):
-            return (k // TENSOR_TILES) * QUAD + k % TENSOR_TILES
+        HALVES = (range(H // 2), range(H // 2, H))
+        MIX_LAG = 3
+        LAST_SLOT = N_TENSOR + 0
+        STEPS = [
+            (w, h, sums)
+            for w in range(N_VECTOR)
+            for h in ((7, 4, 5, 0, 1, 2, 3) if w == 0 else (4, 5, 0, 1, 2, 3))
+            for sums in HALVES
+        ]
+        FIRST_STEPS = 6
+        done = []
+        extra = []
+        taken = []
+        to_fill = []
+        to_transpose = {}
+        to_quantise = {}
+        to_project = {}
+        to_store = {}
+
+        def plan(i, k):
+            to_transpose.setdefault(k, []).append(i)
+            to_quantise.setdefault(k + 1, []).append(i)
+            to_project.setdefault(k + 2, []).append(i)
+            to_store.setdefault(k + 4, []).append(i)
+
+        for k in range(N_TENSOR):
+            plan(tensor_tile(k), k + MIX_LAG + 1)
+
+        def steps_due(k):
+            if k < MIX_LAG:
+                return FIRST_STEPS if k == MIX_LAG - 1 else 0
+            late = (len(STEPS) - FIRST_STEPS) * (k + 1 - MIX_LAG)
+            return min(FIRST_STEPS + late // (LAST_SLOT + 1 - MIX_LAG), len(STEPS))
+
+        def work_on_extra(pieces, k):
+            for piece in extra[len(taken) : len(taken) + pieces]:
+                taken.append(piece)
+                piece(k)
+
+        def multiply(w, h, sums):
+            def piece(k):
+                vector_products(w, h, sums)
+                if w > 0 and h == H - 1 and sums[-1] == H - 1:
+                    vector_join(w)
+            return piece
+
+        def measure_half(w, heads):
+            def piece(k):
+                vector_measure(w, heads)
+                if heads[-1] == H - 1:
+                    vector_normalise(w)
+                    plan(vector_tile(w), k + 1)
+            return piece
+
+        def fill_banks():
+            for w, bank in to_fill:
+                vector_project(w, bank)
+                if bank == 1:
+                    for h in (H - 2, H - 1)[: 1 if w == 0 else 2]:
+                        for sums in HALVES:
+                            extra.append(multiply(w, h, sums))
+            to_fill.clear()
+
+        def step(k):
+            w, h, sums = STEPS[len(done)]
+            while w not in vector_mix:
+                assert len(taken) < len(extra)
+                work_on_extra(1, k)
+            if (w, h // HEADS_PER_BANK) not in vector_v:
+                fill_banks()
+            vector_add_head(w, h, sums)
+            done.append((w, h, sums))
+            if sums[-1] == H - 1 and h == 5 and w + 1 < N_VECTOR:
+                to_fill.append((w + 1, 1))
+            if sums[-1] == H - 1 and h == 3:
+                if w + 1 < N_VECTOR:
+                    to_fill.append((w + 1, 0))
+                for heads in HALVES:
+                    extra.append(measure_half(w, heads))
 
         def is_slot(k):
-            return 0 <= k < N_SLOTS
-
-        def is_quad(q):
-            return 0 <= q < N_QUADS
+            return 0 <= k < N_TENSOR
 
         def slot(k):
-            q, s = divmod(k, TENSOR_TILES)
-            if is_slot(k - 8):
-                add_bias(tensor_tile(k - 8))
-            if s == 2 and is_quad(q - 2):
-                add_bias(vector_tile(q - 2))
+            q_next, step_next = divmod(k + 3, TENSOR_TILES)
+            if step_next < QUAD // PAIR and 2 <= q_next < N_QUADS:
+                transpose_x(q_next, step_next)
+            for i in to_store.get(k, []):
+                store_out(i)
+            if k % TENSOR_TILES == 0 and k // TENSOR_TILES + 2 < N_QUADS:
+                load_x(k // TENSOR_TILES + 2)
+            if is_slot(k - MIX_LAG):
+                mix_on_tensor(k - MIX_LAG, 0)
+                measure(k - MIX_LAG, 0)
+            if is_slot(k - MIX_LAG - 1):
+                normalise(k - MIX_LAG - 1, 1)
+            work_on_extra(3, k)
             if is_slot(k):
-                project_and_park(tensor_tile(k), k)
+                project_and_park(k)
+            for i in to_quantise.get(k, []):
+                quantise_r(i)
+            fill_banks()
             if is_slot(k - 1):
-                fetch_heads(tensor_tile(k - 1), k - 1)
-            if s == 0 and is_quad(q):
-                vector_project(q, 0)
-            if s == 1 and is_quad(q + 1):
-                vector_project(q + 1, 1)
-            if is_slot(k - 4):
-                normalise(tensor_tile(k - 4), 1)
-            if s == 1 and is_quad(q - 2):
-                quantise_r(q - 2)
-            if is_slot(k - 3):
-                mix_on_tensor(tensor_tile(k - 3))
-            if s == 0 and is_quad(q):
-                build_blocks(q)
-            if s == 0 and is_quad(q - 1):
-                vector_measure(q - 1)
-            if s == 1 and is_quad(q + 1):
-                vector_products(q + 1, H - 2)
-            if s == 2 and is_quad(q + 1):
-                vector_products(q + 1, H - 1)
-            if is_quad(q):
-                vector_add_heads(q, ((4, 5), (0, 1), (2, 3))[s])
-            if is_slot(k - 3):
-                measure(tensor_tile(k - 3), 0)
-                normalise(tensor_tile(k - 3), 0)
-                measure(tensor_tile(k - 3), 1)
-            if s == 0 and is_quad(q - 1):
-                vector_normalise(q - 1)
-            if is_slot(k - 4):
-                transpose_r(tensor_tile(k - 4))
-            if s == 1 and is_quad(q - 1):
-                transpose_r(vector_tile(q - 1))
-            if s < QUAD // PAIR and is_quad(q + 2):
-                transpose_x(q + 2, s)
-            if s == 2 and is_quad(q + 2):
-                quantise_x(q + 2)
-            if is_slot(k - 7):
-                project_out(tensor_tile(k - 7))
-            if s == 1 and is_quad(q - 2):
-                project_out(vector_tile(q - 2))
-            if s == 2 and is_quad(q + 1):
-                vector_join(q + 1)
-            if is_slot(k - 9):
-                store_out(tensor_tile(k - 9), k)
-            if s == 0 and is_quad(q - 3):
-                store_out(vector_tile(q - 3), k)
-            if s == 0 and is_quad(q + 3):
-                load_x(q + 3)
+                fetch_heads(k - 1)
+            if is_slot(k - MIX_LAG):
+                mix_on_tensor(k - MIX_LAG, 1)
+            for i in to_project.get(k, []):
+                project_out(i)
+            work_on_extra(2, k)
+            q_built, third = divmod(k + 1, TENSOR_TILES)
+            if 1 <= q_built < N_QUADS:
+                build_blocks(q_built, range(third, GROUP, TENSOR_TILES))
+            if is_slot(k - MIX_LAG):
+                measure(k - MIX_LAG, 1)
+            for i in to_project.get(k, []):
+                add_bias(i)
+            if is_slot(k - MIX_LAG):
+                normalise(k - MIX_LAG, 0)
+            if step_next == QUAD // PAIR and 2 <= q_next < N_QUADS:
+                quantise_x(q_next)
+            while len(done) < steps_due(k):
+                step(k)
+            for i in to_transpose.get(k, []):
+                transpose_r(i)
 
-        FIRST_SLOT = -3 * TENSOR_TILES
-        DIFF_SLOT = -TENSOR_TILES
-        WO_SLOT = 1
-        for k in range(FIRST_SLOT, N_SLOTS + 10):
-            if k == FIRST_SLOT + 1:
-                load_diff()
-                prepare_wv()
-            if k == FIRST_SLOT + TENSOR_TILES + 1:
-                load_wo()
-            if k == DIFF_SLOT:
-                prepare_diff()
-            if k == WO_SLOT:
-                prepare_wo()
-            slot(k)
+        WO_SLOT = 2
+        load_wv(0)
+        load_x(0)
+        load_wv(1)
+        load_vector_diff()
+        load_diff_groups(0)
+        load_x(1)
+        load_wo()
+        load_diff_groups(1)
+        load_x(2)
+        make_constants()
+        transpose_wv(0)
+        transpose_wv(1)
+        transpose_x(0, 0)
+        transpose_x(0, 1)
+        quantise_wv(0)
+        quantise_x(0)
+        transpose_wv(2)
+        transpose_wv(3)
+        quantise_wv(1)
+        project_and_park(0)
+        sort_diff(0)
+        turn_diff(0)
+        nc.vector.tensor_copy(out=vector_diff[:], in_=vector_diff_raw[:])
+        project_and_park(1)
+        fetch_heads(0)
+        build_first_blocks()
+        to_fill.append((0, 1))
+        fill_banks()
+        work_on_extra(2, 0)
+        project_and_park(2)
+        fetch_heads(1)
+        to_fill.append((0, 0))
+        fill_banks()
+        transpose_x(1, 0)
+        transpose_x(1, 1)
+        while len(done) < FIRST_STEPS // 2:
+            step(0)
+        quantise_x(1)
+        while len(done) < FIRST_STEPS:
+            step(0)
+        sort_diff(1)
+        for k in range(MIX_LAG - 1, LAST_SLOT + 12):
+            if k >= MIX_LAG:
+                slot(k)
+            else:
+                build_blocks(1, range(0, GROUP, TENSOR_TILES))
+            if 0 <= k - WO_SLOT < C // P:
+                transpose_wo(k - WO_SLOT)
+            if k == WO_SLOT + C // P - 1:
+                quantise_wo()
+            if k == 6:
+                turn_diff(1)
+        assert len(taken) == len(extra) and len(done) == len(STEPS)

@@ -32,8 +32,6 @@ GROUP = P // H
 GROUPS = P // GROUP
 CLUSTER = 4
 BLOCK_TILES = 2
-PARKING_SLOTS = 4
-FIRST_PARKED = N_TILES - 2 * PARKING_SLOTS
 L0 = 0.8 - 0.6 * math.exp(-0.3 * 12)
 GAIN = 1.0 - L0
 EPS = 1e-5
@@ -179,8 +177,7 @@ def tile_differentialattention_pb_t_kernel(tc, x, diff, Wv, Wo, bo, out):
         r_codes = {}
         acc = {}
         out_sb = {}
-        stored = set()
-        built = {}
+        squares = {}
         normalised = set()
         mixed = set()
 
@@ -241,17 +238,8 @@ def tile_differentialattention_pb_t_kernel(tc, x, diff, Wv, Wo, bo, out):
             q = min(k // TENSOR_TILES, N_QUADS - 1)
             return q * QUAD + k - q * TENSOR_TILES
 
-        def parking_pair(k):
-            pair = k % PARKING_SLOTS
-            return pair if k < N_TENSOR - PARKING_SLOTS else PARKING_SLOTS - 2 + k % 2
-
-        def parking_space(k):
-            first_row = (FIRST_PARKED + 2 * parking_pair(k)) * P
-            return out_rows[first_row : first_row + 2 * P, :].rearrange("r c -> (r c)")
-
-        def project_and_park(k):
+        def project_and_spread(k):
             i = tensor_tile(k)
-            assert not any(FIRST_PARKED + 2 * parking_pair(k) + n in stored for n in range(2))
             v_sb = stage.tile([P, DIM], F32, name="v_sb", bufs=3)
             for bank in range(DIM // BANK):
                 v_bank = psum.tile([P, BANK], F32, tag="misc")
@@ -261,46 +249,34 @@ def tile_differentialattention_pb_t_kernel(tc, x, diff, Wv, Wo, bo, out):
                     nc.scalar.copy(out=v_half, in_=v_bank[:])
                 else:
                     nc.vector.tensor_copy(out=v_half, in_=v_bank[:])
-            nc.sync.dma_start(out=parking_space(k).rearrange("(t w) -> t w", t=P), in_=v_sb[:])
-
-        def fetch_heads(k):
-            i = tensor_tile(k)
             v_heads[i] = stage.tile([P, GROUPS, HD], F32, name="v_heads", bufs=5)
-            nc.sync.dma_start(out=v_heads[i][:], in_=parking_space(k).rearrange("(g p d) -> p g d", g=GROUPS, p=P))
+            for g in range(GROUPS):
+                nc.sync.dma_start(out=v_heads[i][:, g, :], in_=v_sb[g * GROUP : (g + 1) * GROUP, :])
 
         def quad_groups(q):
             return (TENSOR_TILES if q < N_VECTOR else QUAD) * GROUPS
 
-        def build_blocks(q, tokens):
+        def lay_squares(q):
+            squares[q] = stage.tile([P, QUAD * GROUPS, CLUSTER, H], F32, name="squares", bufs=2)
             first = q * QUAD * GROUPS
-            built.setdefault(q, []).extend(tokens)
-            assert q < 2 or ((q - 2) * TENSOR_TILES + 2, 1) in mixed
-            for t in tokens:
-                rows = slice(t * H, (t + 1) * H)
-                nc.sync.dma_start(
-                    out=block_tiles[q % BLOCK_TILES][rows, : quad_groups(q), t, :],
-                    in_=head_weight[rows, first : first + quad_groups(q), :],
-                )
-
-        def build_first_blocks():
-            squares = keep.tile([P, TENSOR_TILES * GROUPS, CLUSTER, H], F32)
             for j in range(CLUSTER):
                 nc.gpsimd.tensor_scalar(
-                    out=squares[:, :, j, :], in0=head_weight[:, : TENSOR_TILES * GROUPS, :],
+                    out=squares[q][:, : quad_groups(q), j, :], in0=head_weight[:, first : first + quad_groups(q), :],
                     scalar1=of_place[:, j : j + 1], scalar2=0.0, op0=ALU.mult, op1=ALU.add,
                 )
-            built[0] = list(range(GROUP))
+
+        def build_blocks(q):
+            assert q < 2 or ((q - 2) * TENSOR_TILES + 2, 1) in mixed
             for c in range(GROUP // CLUSTER):
                 rows = slice(c * CLUSTER * H, (c + 1) * CLUSTER * H)
                 nc.sync.dma_start(
-                    out=block_tiles[0][rows, : TENSOR_TILES * GROUPS, c * CLUSTER : (c + 1) * CLUSTER, :],
-                    in_=squares[rows],
+                    out=block_tiles[q % BLOCK_TILES][rows, : quad_groups(q), c * CLUSTER : (c + 1) * CLUSTER, :],
+                    in_=squares[q][rows, : quad_groups(q)],
                 )
 
         def mix_on_tensor(k, bank):
             i = tensor_tile(k)
             mixed.add((k, bank))
-            assert len(built[i // QUAD]) == GROUP
             mix_banks[(i, bank)] = psum.tile([P, HEADS_PER_BANK, HD], F32, tag="mix", name="mix_bank")
             for s in range(HEADS_PER_BANK):
                 g = bank * HEADS_PER_BANK + s
@@ -423,7 +399,6 @@ def tile_differentialattention_pb_t_kernel(tc, x, diff, Wv, Wo, bo, out):
             nc.gpsimd.tensor_tensor(out=out_sb[i][:], in0=product[:], in1=bias[:], op=ALU.add)
 
         def store_out(i):
-            stored.add(i)
             nc.sync.dma_start(out=out_rows[i * P : (i + 1) * P, :], in_=out_sb[i][:])
 
         HALVES = (range(H // 2), range(H // 2, H))
@@ -524,20 +499,19 @@ def tile_differentialattention_pb_t_kernel(tc, x, diff, Wv, Wo, bo, out):
                 normalise(k - MIX_LAG - 1, 1)
             work_on_extra(3, k)
             if is_slot(k):
-                project_and_park(k)
+                project_and_spread(k)
             for i in to_quantise.get(k, []):
                 quantise_r(i)
             fill_banks()
-            if is_slot(k - 1):
-                fetch_heads(k - 1)
             if is_slot(k - MIX_LAG):
                 mix_on_tensor(k - MIX_LAG, 1)
             for i in to_project.get(k, []):
                 project_out(i)
             work_on_extra(2, k)
-            q_built, third = divmod(k + 1, TENSOR_TILES)
-            if 1 <= q_built < N_QUADS:
-                build_blocks(q_built, range(third, GROUP, TENSOR_TILES))
+            if k % TENSOR_TILES == 1 and k // TENSOR_TILES + 1 < N_QUADS:
+                lay_squares(k // TENSOR_TILES + 1)
+            if k % TENSOR_TILES == 2 and k // TENSOR_TILES + 1 < N_QUADS:
+                build_blocks(k // TENSOR_TILES + 1)
             if is_slot(k - MIX_LAG):
                 measure(k - MIX_LAG, 1)
             for i in to_project.get(k, []):
@@ -571,18 +545,17 @@ def tile_differentialattention_pb_t_kernel(tc, x, diff, Wv, Wo, bo, out):
         transpose_wv(2)
         transpose_wv(3)
         quantise_wv(1)
-        project_and_park(0)
+        project_and_spread(0)
         sort_diff(0)
         turn_diff(0)
         nc.vector.tensor_copy(out=vector_diff[:], in_=vector_diff_raw[:])
-        project_and_park(1)
-        fetch_heads(0)
-        build_first_blocks()
+        project_and_spread(1)
+        lay_squares(0)
+        build_blocks(0)
         to_fill.append((0, 1))
         fill_banks()
         work_on_extra(2, 0)
-        project_and_park(2)
-        fetch_heads(1)
+        project_and_spread(2)
         to_fill.append((0, 0))
         fill_banks()
         transpose_x(1, 0)
@@ -597,7 +570,8 @@ def tile_differentialattention_pb_t_kernel(tc, x, diff, Wv, Wo, bo, out):
             if k >= MIX_LAG:
                 slot(k)
             else:
-                build_blocks(1, range(0, GROUP, TENSOR_TILES))
+                lay_squares(1)
+                build_blocks(1)
             if 0 <= k - WO_SLOT < C // P:
                 transpose_wo(k - WO_SLOT)
             if k == WO_SLOT + C // P - 1:

@@ -96,8 +96,8 @@ def tile_differentialattention_pb_t_kernel(tc, x, diff, Wv, Wo, bo, out):
                 op=ALU.add,
                 axis=mybir.AxisListType.XY,
             )
-            for n in range(BLOCK_TILES):
-                nc.gpsimd.memset(block_tiles[n][:], 0.0)
+            nc.vector.memset(block_tiles[0][:], 0.0)
+            nc.gpsimd.memset(block_tiles[1][:], 0.0)
 
         wv_codes = keep.tile([P, DIM], U32, align_bytes=64)
         wv_scales = keep.tile([P, DIM], U8, align_bytes=64)
@@ -169,7 +169,6 @@ def tile_differentialattention_pb_t_kernel(tc, x, diff, Wv, Wo, bo, out):
         mix_banks = {}
         rms = {}
         vector_v = {}
-        products = {}
         vector_mix = {}
         vector_sumsq = {}
         r = {}
@@ -232,7 +231,11 @@ def tile_differentialattention_pb_t_kernel(tc, x, diff, Wv, Wo, bo, out):
             nc.scalar.activation(
                 out=inv[:], in_=sumsq[:], func=ACT.Abs_reciprocal_sqrt, scale=1.0 / (HD * GAIN * GAIN), bias=eps_term[:]
             )
-            return inv[:].unsqueeze(2).to_broadcast([P, count, HD])
+            return inv
+
+        def scale_heads(out, values, inv, runs):
+            for s in runs:
+                nc.scalar.activation(out=out[:, s, :], in_=values[:, s, :], func=ACT.Copy, scale=inv[:, s : s + 1])
 
         def tensor_tile(k):
             q = min(k // TENSOR_TILES, N_QUADS - 1)
@@ -245,7 +248,7 @@ def tile_differentialattention_pb_t_kernel(tc, x, diff, Wv, Wo, bo, out):
                 v_bank = psum.tile([P, BANK], F32, tag="misc")
                 project_v(i, bank, v_bank[:])
                 v_half = v_sb[:, bank * BANK : (bank + 1) * BANK]
-                if bank == 1 and (k < MIX_LAG or False):
+                if bank == 1:
                     nc.scalar.copy(out=v_half, in_=v_bank[:])
                 else:
                     nc.vector.tensor_copy(out=v_half, in_=v_bank[:])
@@ -259,8 +262,9 @@ def tile_differentialattention_pb_t_kernel(tc, x, diff, Wv, Wo, bo, out):
         def lay_squares(q):
             squares[q] = stage.tile([P, QUAD * GROUPS, CLUSTER, H], F32, name="squares", bufs=2)
             first = q * QUAD * GROUPS
+            engine = nc.vector if q == 0 else nc.gpsimd
             for j in range(CLUSTER):
-                nc.gpsimd.tensor_scalar(
+                engine.tensor_scalar(
                     out=squares[q][:, : quad_groups(q), j, :], in0=head_weight[:, first : first + quad_groups(q), :],
                     scalar1=of_place[:, j : j + 1], scalar2=0.0, op0=ALU.mult, op1=ALU.add,
                 )
@@ -299,12 +303,13 @@ def tile_differentialattention_pb_t_kernel(tc, x, diff, Wv, Wo, bo, out):
             normalised.add((i, bank))
             if bank == 0:
                 r[i] = stage.tile([P, GROUPS, HD], BF16, name="r", bufs=4)
-            nc.vector.tensor_tensor(
-                out=r[i][:, bank * HEADS_PER_BANK : (bank + 1) * HEADS_PER_BANK, :],
-                in0=mix_banks[(i, bank)][:],
-                in1=rms[(i, bank)],
-                op=ALU.mult,
-            )
+            heads = r[i][:, bank * HEADS_PER_BANK : (bank + 1) * HEADS_PER_BANK, :]
+            inv = rms[(i, bank)]
+            if bank == 0 or k % TENSOR_TILES > 0:
+                inv_wide = inv[:].unsqueeze(2).to_broadcast([P, HEADS_PER_BANK, HD])
+                nc.vector.tensor_tensor(out=heads, in0=mix_banks[(i, bank)][:], in1=inv_wide, op=ALU.mult)
+            else:
+                scale_heads(heads, mix_banks[(i, bank)], inv, range(HEADS_PER_BANK))
 
         def vector_tile(w):
             return w * QUAD + QUAD - 1
@@ -320,20 +325,14 @@ def tile_differentialattention_pb_t_kernel(tc, x, diff, Wv, Wo, bo, out):
             vector_v[(w, bank)] = psum.tile([P, BANK], F32, tag="vector_v%d" % bank, bufs=1, name="vector_v")
             project_v(vector_tile(w), bank, vector_v[(w, bank)][:])
 
-        def vector_products(w, h, sums):
-            if w == 0 and w not in vector_mix:
+        def vector_products(w, sums):
+            if w not in vector_mix:
                 vector_mix[w] = stage.tile([P, H, HD], F32, name="vector_mix", bufs=2)
-            if w > 0 and w not in products:
-                products[w] = stage.tile([P, 2, H, HD], F32, name="products", bufs=2)
             for a in sums:
                 nc.scalar.activation(
-                    out=vector_mix[w][:, a, :] if w == 0 else products[w][:, h - (H - 2), a, :],
-                    in_=vector_head(w, h), func=ACT.Copy, scale=vector_weight(w, a, h),
+                    out=vector_mix[w][:, a, :], in_=vector_head(w, H - 1), func=ACT.Copy,
+                    scale=vector_weight(w, a, H - 1),
                 )
-
-        def vector_join(w):
-            vector_mix[w] = stage.tile([P, H, HD], F32, name="vector_mix", bufs=2)
-            nc.gpsimd.tensor_tensor(out=vector_mix[w][:], in0=products[w][:, 0], in1=products[w][:, 1], op=ALU.add)
 
         def vector_add_head(w, h, sums):
             for a in sums:
@@ -347,11 +346,12 @@ def tile_differentialattention_pb_t_kernel(tc, x, diff, Wv, Wo, bo, out):
                 vector_sumsq[w] = stage.tile([P, H], F32, name="vector_sumsq")
             squares_of(vector_mix[w], vector_sumsq[w], heads)
 
-        def vector_normalise(w):
+        def vector_normalise(w, heads):
             i = vector_tile(w)
-            rms[i] = inverse_rms(vector_sumsq[w], H)
-            r[i] = stage.tile([P, H, HD], BF16, name="r", bufs=4)
-            nc.gpsimd.tensor_tensor(out=r[i][:], in0=vector_mix[w][:], in1=rms[i], op=ALU.mult)
+            if i not in rms:
+                rms[i] = inverse_rms(vector_sumsq[w], H)
+                r[i] = stage.tile([P, H, HD], BF16, name="r", bufs=4)
+            scale_heads(r[i], vector_mix[w], rms[i], heads)
 
         def transpose_r(i):
             r_t = psum.tile([P, H * P], BF16, tag="misc")
@@ -389,14 +389,8 @@ def tile_differentialattention_pb_t_kernel(tc, x, diff, Wv, Wo, bo, out):
                 )
 
         def add_bias(i):
-            if i >= N_TILES - 2:
-                out_sb[i] = stage.tile([P, C], F32, name="out_sb", bufs=4)
-                nc.vector.tensor_tensor(out=out_sb[i][:], in0=acc[i][:], in1=bias[:], op=ALU.add)
-                return
-            product = stage.tile([P, C], F32, name="product")
-            nc.scalar.copy(out=product[:], in_=acc[i][:])
             out_sb[i] = stage.tile([P, C], F32, name="out_sb", bufs=4)
-            nc.gpsimd.tensor_tensor(out=out_sb[i][:], in0=product[:], in1=bias[:], op=ALU.add)
+            nc.vector.tensor_tensor(out=out_sb[i][:], in0=acc[i][:], in1=bias[:], op=ALU.add)
 
         def store_out(i):
             nc.sync.dma_start(out=out_rows[i * P : (i + 1) * P, :], in_=out_sb[i][:])
@@ -407,11 +401,12 @@ def tile_differentialattention_pb_t_kernel(tc, x, diff, Wv, Wo, bo, out):
         STEPS = [
             (w, h, sums)
             for w in range(N_VECTOR)
-            for h in ((7, 4, 5, 0, 1, 2, 3) if w == 0 else (4, 5, 0, 1, 2, 3))
+            for h in (6, 4, 5, 0, 1, 2, 3)
             for sums in HALVES
         ]
-        FIRST_STEPS = 6
+        FIRST_STEPS = 4
         done = []
+        started = []
         extra = []
         taken = []
         to_fill = []
@@ -424,7 +419,7 @@ def tile_differentialattention_pb_t_kernel(tc, x, diff, Wv, Wo, bo, out):
             to_transpose.setdefault(k, []).append(i)
             to_quantise.setdefault(k + 1, []).append(i)
             to_project.setdefault(k + 2, []).append(i)
-            to_store.setdefault(k + 4, []).append(i)
+            to_store.setdefault(k + 3, []).append(i)
 
         for k in range(N_TENSOR):
             plan(tensor_tile(k), k + MIX_LAG + 1)
@@ -440,18 +435,22 @@ def tile_differentialattention_pb_t_kernel(tc, x, diff, Wv, Wo, bo, out):
                 taken.append(piece)
                 piece(k)
 
-        def multiply(w, h, sums):
+        def multiply(w, sums):
             def piece(k):
-                vector_products(w, h, sums)
-                if w > 0 and h == H - 1 and sums[-1] == H - 1:
-                    vector_join(w)
+                vector_products(w, sums)
+                if sums[-1] == H - 1:
+                    started.append(w)
             return piece
 
         def measure_half(w, heads):
             def piece(k):
                 vector_measure(w, heads)
+            return piece
+
+        def normalise_half(w, heads):
+            def piece(k):
+                vector_normalise(w, heads)
                 if heads[-1] == H - 1:
-                    vector_normalise(w)
                     plan(vector_tile(w), k + 1)
             return piece
 
@@ -459,14 +458,13 @@ def tile_differentialattention_pb_t_kernel(tc, x, diff, Wv, Wo, bo, out):
             for w, bank in to_fill:
                 vector_project(w, bank)
                 if bank == 1:
-                    for h in (H - 2, H - 1)[: 1 if w == 0 else 2]:
-                        for sums in HALVES:
-                            extra.append(multiply(w, h, sums))
+                    for sums in HALVES:
+                        extra.append(multiply(w, sums))
             to_fill.clear()
 
         def step(k):
             w, h, sums = STEPS[len(done)]
-            while w not in vector_mix:
+            while len(started) <= w:
                 assert len(taken) < len(extra)
                 work_on_extra(1, k)
             if (w, h // HEADS_PER_BANK) not in vector_v:
@@ -478,52 +476,50 @@ def tile_differentialattention_pb_t_kernel(tc, x, diff, Wv, Wo, bo, out):
             if sums[-1] == H - 1 and h == 3:
                 if w + 1 < N_VECTOR:
                     to_fill.append((w + 1, 0))
-                for heads in HALVES:
-                    extra.append(measure_half(w, heads))
+                for piece in (measure_half, normalise_half):
+                    for heads in HALVES:
+                        extra.append(piece(w, heads))
 
         def is_slot(k):
             return 0 <= k < N_TENSOR
 
         def slot(k):
+            if is_slot(k - MIX_LAG):
+                mix_on_tensor(k - MIX_LAG, 0)
+                measure(k - MIX_LAG, 0)
             q_next, step_next = divmod(k + 3, TENSOR_TILES)
             if step_next < QUAD // PAIR and 2 <= q_next < N_QUADS:
                 transpose_x(q_next, step_next)
+            if is_slot(k):
+                project_and_spread(k)
+            if is_slot(k - MIX_LAG - 1):
+                normalise(k - MIX_LAG - 1, 1)
             for i in to_store.get(k, []):
                 store_out(i)
             if k % TENSOR_TILES == 0 and k // TENSOR_TILES + 2 < N_QUADS:
                 load_x(k // TENSOR_TILES + 2)
-            if is_slot(k - MIX_LAG):
-                mix_on_tensor(k - MIX_LAG, 0)
-                measure(k - MIX_LAG, 0)
-            if is_slot(k - MIX_LAG - 1):
-                normalise(k - MIX_LAG - 1, 1)
-            work_on_extra(3, k)
-            if is_slot(k):
-                project_and_spread(k)
+            if step_next == QUAD // PAIR and 2 <= q_next < N_QUADS:
+                quantise_x(q_next)
             for i in to_quantise.get(k, []):
                 quantise_r(i)
-            fill_banks()
+            work_on_extra(2, k)
             if is_slot(k - MIX_LAG):
                 mix_on_tensor(k - MIX_LAG, 1)
-            for i in to_project.get(k, []):
-                project_out(i)
-            work_on_extra(2, k)
+                normalise(k - MIX_LAG, 0)
             if k % TENSOR_TILES == 1 and k // TENSOR_TILES + 1 < N_QUADS:
                 lay_squares(k // TENSOR_TILES + 1)
             if k % TENSOR_TILES == 2 and k // TENSOR_TILES + 1 < N_QUADS:
                 build_blocks(k // TENSOR_TILES + 1)
             if is_slot(k - MIX_LAG):
                 measure(k - MIX_LAG, 1)
+            fill_banks()
             for i in to_project.get(k, []):
+                project_out(i)
                 add_bias(i)
-            if is_slot(k - MIX_LAG):
-                normalise(k - MIX_LAG, 0)
-            if step_next == QUAD // PAIR and 2 <= q_next < N_QUADS:
-                quantise_x(q_next)
-            while len(done) < steps_due(k):
-                step(k)
             for i in to_transpose.get(k, []):
                 transpose_r(i)
+            while len(done) < steps_due(k):
+                step(k)
 
         WO_SLOT = 2
         load_wv(0)
@@ -549,9 +545,9 @@ def tile_differentialattention_pb_t_kernel(tc, x, diff, Wv, Wo, bo, out):
         sort_diff(0)
         turn_diff(0)
         nc.vector.tensor_copy(out=vector_diff[:], in_=vector_diff_raw[:])
-        project_and_spread(1)
         lay_squares(0)
         build_blocks(0)
+        project_and_spread(1)
         to_fill.append((0, 1))
         fill_banks()
         work_on_extra(2, 0)

@@ -165,8 +165,10 @@ def tile_differentialattention_pb_t_kernel(tc, x, diff, Wv, Wo, bo, out):
         x_raw = {}
         x_grouped = {}
         x_codes = {}
+        v_sb = {}
         v_heads = {}
         mix_banks = {}
+        bank_sumsq = {}
         rms = {}
         vector_v = {}
         vector_mix = {}
@@ -243,18 +245,30 @@ def tile_differentialattention_pb_t_kernel(tc, x, diff, Wv, Wo, bo, out):
 
         def project_and_spread(k):
             i = tensor_tile(k)
-            v_sb = stage.tile([P, DIM], F32, name="v_sb", bufs=3)
+            pair, j = divmod(k + 1, PAIR)
+            if pair not in v_sb:
+                v_sb[pair] = stage.tile([P, H, PAIR, HD], F32, name="v_sb", bufs=2)
             for bank in range(DIM // BANK):
-                v_bank = psum.tile([P, BANK], F32, tag="misc")
-                project_v(i, bank, v_bank[:])
-                v_half = v_sb[:, bank * BANK : (bank + 1) * BANK]
+                v_bank = psum.tile([P, HEADS_PER_BANK, HD], F32, tag="misc")
+                project_v(i, bank, v_bank[:].rearrange("p h d -> p (h d)"))
+                v_half = v_sb[pair][:, bank * HEADS_PER_BANK : (bank + 1) * HEADS_PER_BANK, j, :]
                 if bank == 1:
                     nc.scalar.copy(out=v_half, in_=v_bank[:])
                 else:
                     nc.vector.tensor_copy(out=v_half, in_=v_bank[:])
-            v_heads[i] = stage.tile([P, GROUPS, HD], F32, name="v_heads", bufs=5)
-            for g in range(GROUPS):
-                nc.sync.dma_start(out=v_heads[i][:, g, :], in_=v_sb[g * GROUP : (g + 1) * GROUP, :])
+            if j == PAIR - 1 and k > 0:
+                v_heads[pair] = stage.tile([P, GROUPS, PAIR, HD], F32, name="v_heads")
+                for g in range(GROUPS):
+                    nc.sync.dma_start(
+                        out=v_heads[pair][:, g].rearrange("p j d -> p (j d)"),
+                        in_=v_sb[pair][g * GROUP : (g + 1) * GROUP].rearrange("t h j d -> t (h j d)"),
+                    )
+            elif k == 0:
+                v_heads[pair] = stage.tile([P, GROUPS, PAIR, HD], F32, name="v_heads")
+                for g in range(GROUPS):
+                    nc.sync.dma_start(
+                        out=v_heads[pair][:, g, j, :], in_=v_sb[pair][g * GROUP : (g + 1) * GROUP, :, j, :]
+                    )
 
         def quad_groups(q):
             return (TENSOR_TILES if q < N_VECTOR else QUAD) * GROUPS
@@ -287,16 +301,19 @@ def tile_differentialattention_pb_t_kernel(tc, x, diff, Wv, Wo, bo, out):
                 nc.tensor.matmul(
                     out=mix_banks[(i, bank)][:, s, :],
                     lhsT=block_tiles[(i // QUAD) % BLOCK_TILES][:, (i % QUAD) * GROUPS + g].rearrange("p t a -> p (t a)"),
-                    rhs=v_heads[i][:, g, :],
+                    rhs=v_heads[(k + 1) // PAIR][:, g, (k + 1) % PAIR, :],
                     start=True,
                     stop=True,
                 )
 
         def measure(k, bank):
             i = tensor_tile(k)
-            sumsq = stage.tile([P, HEADS_PER_BANK], F32, name="sumsq")
-            squares_of(mix_banks[(i, bank)], sumsq, range(HEADS_PER_BANK))
-            rms[(i, bank)] = inverse_rms(sumsq, HEADS_PER_BANK)
+            bank_sumsq[(i, bank)] = stage.tile([P, HEADS_PER_BANK], F32, name="sumsq")
+            squares_of(mix_banks[(i, bank)], bank_sumsq[(i, bank)], range(HEADS_PER_BANK))
+
+        def invert(k, bank):
+            i = tensor_tile(k)
+            rms[(i, bank)] = inverse_rms(bank_sumsq[(i, bank)], HEADS_PER_BANK)
 
         def normalise(k, bank):
             i = tensor_tile(k)
@@ -305,7 +322,7 @@ def tile_differentialattention_pb_t_kernel(tc, x, diff, Wv, Wo, bo, out):
                 r[i] = stage.tile([P, GROUPS, HD], BF16, name="r", bufs=4)
             heads = r[i][:, bank * HEADS_PER_BANK : (bank + 1) * HEADS_PER_BANK, :]
             inv = rms[(i, bank)]
-            if bank == 0 or k % TENSOR_TILES > 0:
+            if bank == 0 or k % 2 > 0:
                 inv_wide = inv[:].unsqueeze(2).to_broadcast([P, HEADS_PER_BANK, HD])
                 nc.vector.tensor_tensor(out=heads, in0=mix_banks[(i, bank)][:], in1=inv_wide, op=ALU.mult)
             else:
@@ -346,12 +363,11 @@ def tile_differentialattention_pb_t_kernel(tc, x, diff, Wv, Wo, bo, out):
                 vector_sumsq[w] = stage.tile([P, H], F32, name="vector_sumsq")
             squares_of(vector_mix[w], vector_sumsq[w], heads)
 
-        def vector_normalise(w, heads):
+        def vector_normalise(w):
             i = vector_tile(w)
-            if i not in rms:
-                rms[i] = inverse_rms(vector_sumsq[w], H)
-                r[i] = stage.tile([P, H, HD], BF16, name="r", bufs=4)
-            scale_heads(r[i], vector_mix[w], rms[i], heads)
+            inv_wide = inverse_rms(vector_sumsq[w], H)[:].unsqueeze(2).to_broadcast([P, H, HD])
+            r[i] = stage.tile([P, H, HD], BF16, name="r", bufs=4)
+            nc.gpsimd.tensor_tensor(out=r[i][:], in0=vector_mix[w][:], in1=inv_wide, op=ALU.mult)
 
         def transpose_r(i):
             r_t = psum.tile([P, H * P], BF16, tag="misc")
@@ -363,7 +379,8 @@ def tile_differentialattention_pb_t_kernel(tc, x, diff, Wv, Wo, bo, out):
             else:
                 by_pass = r_t[:].rearrange("p (t q j) -> p q t j", q=2, j=PACK)
             r_grouped[i] = stage.tile([P, 2, P, PACK], BF16, align_bytes=64, name="r_grouped", bufs=3)
-            nc.scalar.copy(out=r_grouped[i][:], in_=by_pass)
+            copy = nc.vector.tensor_copy if i >= N_TILES - 3 else nc.scalar.copy
+            copy(out=r_grouped[i][:], in_=by_pass)
 
         def quantise_r(i):
             codes = stage.tile([P, 2 * P], U32, align_bytes=64, name="r_codes", bufs=3)
@@ -447,11 +464,10 @@ def tile_differentialattention_pb_t_kernel(tc, x, diff, Wv, Wo, bo, out):
                 vector_measure(w, heads)
             return piece
 
-        def normalise_half(w, heads):
+        def finish(w):
             def piece(k):
-                vector_normalise(w, heads)
-                if heads[-1] == H - 1:
-                    plan(vector_tile(w), k + 1)
+                vector_normalise(w)
+                plan(vector_tile(w), k + 1)
             return piece
 
         def fill_banks():
@@ -476,9 +492,9 @@ def tile_differentialattention_pb_t_kernel(tc, x, diff, Wv, Wo, bo, out):
             if sums[-1] == H - 1 and h == 3:
                 if w + 1 < N_VECTOR:
                     to_fill.append((w + 1, 0))
-                for piece in (measure_half, normalise_half):
-                    for heads in HALVES:
-                        extra.append(piece(w, heads))
+                for heads in HALVES:
+                    extra.append(measure_half(w, heads))
+                extra.append(finish(w))
 
         def is_slot(k):
             return 0 <= k < N_TENSOR
@@ -492,6 +508,8 @@ def tile_differentialattention_pb_t_kernel(tc, x, diff, Wv, Wo, bo, out):
                 transpose_x(q_next, step_next)
             if is_slot(k):
                 project_and_spread(k)
+            if is_slot(k - MIX_LAG):
+                invert(k - MIX_LAG, 0)
             if is_slot(k - MIX_LAG - 1):
                 normalise(k - MIX_LAG - 1, 1)
             for i in to_store.get(k, []):
@@ -518,6 +536,8 @@ def tile_differentialattention_pb_t_kernel(tc, x, diff, Wv, Wo, bo, out):
                 add_bias(i)
             for i in to_transpose.get(k, []):
                 transpose_r(i)
+            if is_slot(k - MIX_LAG):
+                invert(k - MIX_LAG, 1)
             while len(done) < steps_due(k):
                 step(k)
 

import math
from contextlib import ExitStack

import concourse.mybir as mybir
from concourse.masks import make_identity

F32 = mybir.dt.float32
BF16 = mybir.dt.bfloat16
U32 = mybir.dt.uint32
U8 = mybir.dt.uint8
FP8X4 = mybir.dt.float8_e4m3fn_x4
ACT = mybir.ActivationFunctionType
ALU = mybir.AluOpType

P = 128
PACK = 4
TOKENS = 4 * 1024
C = 512
DIM = 1024
H = 8
HD = DIM // H
BANK = 512
HEADS_PER_BANK = BANK // HD
N_TILES = TOKENS // P
QUAD = 4
N_QUADS = N_TILES // QUAD
N_VECTOR = N_QUADS - 1
N_TENSOR = N_TILES - N_VECTOR
TENSOR_TILES = QUAD - 1
PAIR = 2
GROUP = P // H
GROUPS = P // GROUP
CLUSTER = 4
BLOCK_TILES = 2
L0 = 0.8 - 0.6 * math.exp(-0.3 * 12)
GAIN = 1.0 - L0
EPS = 1e-5

FLOPS = 2 * TOKENS * C * DIM * 2 + 2 * TOKENS * H * H * HD


def tile_differentialattention_pb_t_kernel(tc, x, diff, Wv, Wo, bo, out):
    nc = tc.nc
    x_rows = x.flatten_outer_dims()
    diff_rows = diff.rearrange("b n a h -> (b n) (a h)")
    out_rows = out.flatten_outer_dims()

    with ExitStack() as stack:
        keep = stack.enter_context(tc.tile_pool(name="keep", bufs=1))
        stage = stack.enter_context(tc.tile_pool(name="stage", bufs=3))
        psum = stack.enter_context(tc.psum_pool(name="psum", bufs=3))
        stack.enter_context(tc.manual_schedule())

        wv_raw = keep.tile([P, DIM // P, C], BF16)
        vector_diff_raw = keep.tile([P, N_QUADS, H * H], BF16)
        diff_groups = keep.tile([P, 2, GROUP * H * H], BF16)
        wo_raw = keep.tile([P, C // P, DIM], BF16)
        bias_raw = keep.tile([P, C], BF16)

        def load_wv(half):
            rows = slice(half * DIM // 2, (half + 1) * DIM // 2)
            tiles = slice(half * DIM // P // 2, (half + 1) * DIM // P // 2)
            nc.sync.dma_start(out=wv_raw[:, tiles, :], in_=Wv[rows, :].rearrange("(r p) k -> p r k", p=P))

        def load_vector_diff():
            nc.sync.dma_start(
                out=vector_diff_raw[:],
                in_=diff_rows.rearrange("(q s p) c -> p q s c", s=QUAD, p=P)[:, :, QUAD - 1, :],
            )

        def load_diff_groups(y):
            rows = slice(y * TOKENS // 2, (y + 1) * TOKENS // 2)
            nc.sync.dma_start(out=diff_groups[:, y, :], in_=diff_rows[rows, :].rearrange("(g t) c -> g (t c)", t=GROUP))

        def load_wo():
            nc.sync.dma_start(out=wo_raw[:], in_=Wo.rearrange("(r p) k -> p r k", p=P))
            nc.sync.dma_start(out=bias_raw[:], in_=bo.partition_broadcast(P))

        ident_f32 = keep.tile([P, P], F32)
        ident_bf16 = keep.tile([P, P], BF16)
        of_place = keep.tile([P, CLUSTER], F32)
        eps_term = keep.tile([P, 1], F32)
        block_tiles = []
        for n in range(BLOCK_TILES):
            block_tiles.append(keep.tile([P, QUAD * GROUPS, GROUP, H], F32, name="blocks%d" % n))

        def make_constants():
            make_identity(nc, ident_f32[:])
            make_identity(nc, ident_bf16[:])
            nc.vector.tensor_scalar(
                out=eps_term[:], in0=ident_f32[:, 0:1], scalar1=0.0, scalar2=EPS / (GAIN * GAIN), op0=ALU.mult, op1=ALU.add
            )
            nc.vector.tensor_reduce(
                out=of_place[:],
                in_=ident_f32[:].rearrange("p (c j h) -> p j c h", j=CLUSTER, h=H),
                op=ALU.add,
                axis=mybir.AxisListType.XY,
            )
            nc.vector.memset(block_tiles[0][:], 0.0)
            nc.gpsimd.memset(block_tiles[1][:], 0.0)

        wv_codes = keep.tile([P, DIM], U32, align_bytes=64)
        wv_scales = keep.tile([P, DIM], U8, align_bytes=64)
        wo_codes = keep.tile([P, 2 * C], U32, align_bytes=64)
        wo_scales = keep.tile([P, 2 * C], U8, align_bytes=64)
        vector_diff = keep.tile([P, N_QUADS, H * H], F32)
        head_weight = keep.tile([P, 2 * P, H], F32)
        bias = keep.tile([P, C], F32)
        wv_grouped = keep.tile([P, DIM * PACK], BF16, align_bytes=64, name="wv_grouped", tag="w_grouped")

        def transpose_wv(pair):
            grouped_words = wv_grouped[:].bitcast(F32).rearrange("p (s w u) -> p s w u", w=P, u=2)
            wv_t = psum.tile([P, PAIR, 2, P], F32, tag="mix")
            for s in range(PAIR):
                words = wv_raw[:, pair * PAIR + s, :].bitcast(F32)
                for u in range(2):
                    nc.tensor.transpose(wv_t[:, s, u, :], words[:, u * P : (u + 1) * P], ident_f32[:])
            out_words = grouped_words[:, pair * PAIR : (pair + 1) * PAIR]
            in_words = wv_t[:].rearrange("p s u w -> p s w u")
            if pair % 2 == 0:
                nc.vector.tensor_copy(out=out_words, in_=in_words)
            else:
                nc.scalar.copy(out=out_words, in_=in_words)

        def quantise_wv(half):
            cols = slice(half * DIM // 2, (half + 1) * DIM // 2)
            vals = slice(half * DIM * PACK // 2, (half + 1) * DIM * PACK // 2)
            nc.vector.quantize_mx(
                out=wv_codes[:, cols].bitcast(FP8X4), scales=wv_scales[:, cols], in_=wv_grouped[:, vals]
            )

        diff_by_a = keep.tile([P, 2, H, GROUP, H], BF16)

        def sort_diff(y):
            nc.vector.tensor_copy(
                out=diff_by_a[:, y], in_=diff_groups[:, y, :].rearrange("p (t a h) -> p a t h", a=H, h=H)
            )

        def turn_diff(y):
            diff_t = psum.tile([P, H, P], BF16, tag="misc")
            for a in range(H):
                nc.tensor.transpose(
                    diff_t[:, a, :], diff_by_a[:, y, a].rearrange("p t h -> p (t h)"), ident_bf16[:]
                )
            nc.scalar.copy(out=head_weight[:, y * P : (y + 1) * P, :], in_=diff_t[:].rearrange("p a g -> p g a"))

        wo_grouped = []

        def transpose_wo(r):
            if r == 0:
                wo_grouped.append(keep.tile([P, 2, C, PACK], BF16, align_bytes=64, name="wo_grouped", tag="w_grouped"))
            wo_t = psum.tile([P, H, P], BF16, tag="misc")
            for a in range(H):
                nc.tensor.transpose(wo_t[:, a, :], wo_raw[:, r, a * HD : (a + 1) * HD], ident_bf16[:])
            nc.scalar.copy(
                out=wo_grouped[0][:, :, r * P : (r + 1) * P, :], in_=wo_t[:].rearrange("p (g j) c -> p g c j", j=PACK)
            )

        def quantise_wo():
            nc.vector.quantize_mx(
                out=wo_codes[:].bitcast(FP8X4), scales=wo_scales[:], in_=wo_grouped[0][:].rearrange("p g c j -> p (g c j)")
            )
            nc.vector.tensor_copy(out=bias[:], in_=bias_raw[:])

        x_raw = {}
        x_grouped = {}
        x_codes = {}
        v_sb = {}
        v_heads = {}
        mix_banks = {}
        bank_sumsq = {}
        rms = {}
        vector_v = {}
        vector_mix = {}
        vector_sumsq = {}
        r = {}
        r_grouped = {}
        r_codes = {}
        acc = {}
        out_sb = {}
        squares = {}
        normalised = set()
        mixed = set()

        def is_vector(i):
            return i % QUAD == QUAD - 1 and i // QUAD < N_VECTOR

        def load_x(q):
            x_raw[q] = stage.tile([P, QUAD, C], BF16, name="x_raw")
            nc.sync.dma_start(
                out=x_raw[q][:], in_=x_rows[q * QUAD * P : (q + 1) * QUAD * P, :].rearrange("(s p) k -> p s k", p=P)
            )

        def transpose_x(q, pair):
            if q not in x_grouped:
                x_grouped[q] = stage.tile([P, QUAD * P * PACK], BF16, align_bytes=64, name="x_grouped", bufs=2)
            grouped_words = x_grouped[q][:].bitcast(F32).rearrange("p (s t u) -> p s t u", t=P, u=2)
            x_t = psum.tile([P, PAIR, 2, P], F32, tag="misc")
            for s in range(PAIR):
                words = x_raw[q][:, pair * PAIR + s, :].bitcast(F32)
                for u in range(2):
                    nc.tensor.transpose(x_t[:, s, u, :], words[:, u * P : (u + 1) * P], ident_f32[:])
            copy = nc.vector.tensor_copy if (q, pair) == (0, 1) else nc.scalar.copy
            copy(out=grouped_words[:, pair * PAIR : (pair + 1) * PAIR], in_=x_t[:].rearrange("p s u t -> p s t u"))

        def quantise_x(q):
            codes = stage.tile([P, QUAD * P], U32, align_bytes=64, name="x_codes")
            scales = stage.tile([P, QUAD * P], U8, align_bytes=64, name="x_scales")
            nc.vector.quantize_mx(out=codes[:].bitcast(FP8X4), scales=scales[:], in_=x_grouped[q][:])
            x_codes[q] = (codes, scales)

        def project_v(i, bank, v_bank):
            codes, scales = x_codes[i // QUAD]
            tok = slice((i % QUAD) * P, (i % QUAD + 1) * P)
            cols = slice(bank * BANK, (bank + 1) * BANK)
            nc.tensor.matmul_mx(
                out=v_bank,
                lhsT=codes[:, tok].bitcast(FP8X4),
                lhsT_scale=scales[:, tok],
                rhs=wv_codes[:, cols].bitcast(FP8X4),
                rhs_scale=wv_scales[:, cols],
                start=True,
                stop=True,
            )

        def squares_of(values, sumsq, runs):
            for s in runs:
                square = stage.tile([P, HD], BF16, name="square")
                nc.scalar.activation(out=square[:], in_=values[:, s, :], func=ACT.Square, accum_out=sumsq[:, s : s + 1])

        def inverse_rms(sumsq, count):
            inv = stage.tile([P, count], F32, name="inv", bufs=6)
            nc.scalar.activation(
                out=inv[:], in_=sumsq[:], func=ACT.Abs_reciprocal_sqrt, scale=1.0 / (HD * GAIN * GAIN), bias=eps_term[:]
            )
            return inv

        def scale_heads(out, values, inv, runs):
            for s in runs:
                nc.scalar.activation(out=out[:, s, :], in_=values[:, s, :], func=ACT.Copy, scale=inv[:, s : s + 1])

        def tensor_tile(k):
            q = min(k // TENSOR_TILES, N_QUADS - 1)
            return q * QUAD + k - q * TENSOR_TILES

        def project_and_spread(k):
            i = tensor_tile(k)
            pair, j = divmod(k + 1, PAIR)
            if pair not in v_sb:
                v_sb[pair] = stage.tile([P, H, PAIR, HD], F32, name="v_sb", bufs=2)
            for bank in range(DIM // BANK):
                v_bank = psum.tile([P, HEADS_PER_BANK, HD], F32, tag="misc")
                project_v(i, bank, v_bank[:].rearrange("p h d -> p (h d)"))
                v_half = v_sb[pair][:, bank * HEADS_PER_BANK : (bank + 1) * HEADS_PER_BANK, j, :]
                if bank == 1:
                    nc.scalar.copy(out=v_half, in_=v_bank[:])
                else:
                    nc.vector.tensor_copy(out=v_half, in_=v_bank[:])
            if j == PAIR - 1 and k > 0:
                v_heads[pair] = stage.tile([P, GROUPS, PAIR, HD], F32, name="v_heads")
                for g in range(GROUPS):
                    nc.sync.dma_start(
                        out=v_heads[pair][:, g].rearrange("p j d -> p (j d)"),
                        in_=v_sb[pair][g * GROUP : (g + 1) * GROUP].rearrange("t h j d -> t (h j d)"),
                    )
            elif k == 0:
                v_heads[pair] = stage.tile([P, GROUPS, PAIR, HD], F32, name="v_heads")
                for g in range(GROUPS):
                    nc.sync.dma_start(
                        out=v_heads[pair][:, g, j, :], in_=v_sb[pair][g * GROUP : (g + 1) * GROUP, :, j, :]
                    )

        def quad_groups(q):
            return (TENSOR_TILES if q < N_VECTOR else QUAD) * GROUPS

        def lay_squares(q):
            squares[q] = stage.tile([P, QUAD * GROUPS, CLUSTER, H], F32, name="squares", bufs=2)
            first = q * QUAD * GROUPS
            engine = nc.vector if q == 0 else nc.gpsimd
            for j in range(CLUSTER):
                engine.tensor_scalar(
                    out=squares[q][:, : quad_groups(q), j, :], in0=head_weight[:, first : first + quad_groups(q), :],
                    scalar1=of_place[:, j : j + 1], scalar2=0.0, op0=ALU.mult, op1=ALU.add,
                )

        def build_blocks(q):
            assert q < 2 or ((q - 2) * TENSOR_TILES + 2, 1) in mixed
            for c in range(GROUP // CLUSTER):
                rows = slice(c * CLUSTER * H, (c + 1) * CLUSTER * H)
                nc.sync.dma_start(
                    out=block_tiles[q % BLOCK_TILES][rows, : quad_groups(q), c * CLUSTER : (c + 1) * CLUSTER, :],
                    in_=squares[q][rows, : quad_groups(q)],
                )

        def mix_on_tensor(k, bank):
            i = tensor_tile(k)
            mixed.add((k, bank))
            mix_banks[(i, bank)] = psum.tile([P, HEADS_PER_BANK, HD], F32, tag="mix", name="mix_bank")
            for s in range(HEADS_PER_BANK):
                g = bank * HEADS_PER_BANK + s
                nc.tensor.matmul(
                    out=mix_banks[(i, bank)][:, s, :],
                    lhsT=block_tiles[(i // QUAD) % BLOCK_TILES][:, (i % QUAD) * GROUPS + g].rearrange("p t a -> p (t a)"),
                    rhs=v_heads[(k + 1) // PAIR][:, g, (k + 1) % PAIR, :],
                    start=True,
                    stop=True,
                )

        def measure(k, bank):
            i = tensor_tile(k)
            bank_sumsq[(i, bank)] = stage.tile([P, HEADS_PER_BANK], F32, name="sumsq")
            squares_of(mix_banks[(i, bank)], bank_sumsq[(i, bank)], range(HEADS_PER_BANK))

        def invert(k, bank):
            i = tensor_tile(k)
            rms[(i, bank)] = inverse_rms(bank_sumsq[(i, bank)], HEADS_PER_BANK)

        def normalise(k, bank):
            i = tensor_tile(k)
            normalised.add((i, bank))
            if bank == 0:
                r[i] = stage.tile([P, GROUPS, HD], BF16, name="r", bufs=4)
            heads = r[i][:, bank * HEADS_PER_BANK : (bank + 1) * HEADS_PER_BANK, :]
            inv = rms[(i, bank)]
            if bank == 0 or k % 2 > 0:
                inv_wide = inv[:].unsqueeze(2).to_broadcast([P, HEADS_PER_BANK, HD])
                nc.vector.tensor_tensor(out=heads, in0=mix_banks[(i, bank)][:], in1=inv_wide, op=ALU.mult)
            else:
                scale_heads(heads, mix_banks[(i, bank)], inv, range(HEADS_PER_BANK))

        def vector_tile(w):
            return w * QUAD + QUAD - 1

        def vector_weight(w, a, h):
            return vector_diff[:, w, a * H + h : a * H + h + 1]

        def vector_head(w, h):
            col = (h % HEADS_PER_BANK) * HD
            return vector_v[(w, h // HEADS_PER_BANK)][:, col : col + HD]

        def vector_project(w, bank):
            vector_v[(w, bank)] = psum.tile([P, BANK], F32, tag="vector_v%d" % bank, bufs=1, name="vector_v")
            project_v(vector_tile(w), bank, vector_v[(w, bank)][:])

        def vector_products(w, sums):
            if w not in vector_mix:
                vector_mix[w] = stage.tile([P, H, HD], F32, name="vector_mix", bufs=2)
            for a in sums:
                nc.scalar.activation(
                    out=vector_mix[w][:, a, :], in_=vector_head(w, H - 1), func=ACT.Copy,
                    scale=vector_weight(w, a, H - 1),
                )

        def vector_add_head(w, h, sums):
            for a in sums:
                nc.vector.scalar_tensor_tensor(
                    out=vector_mix[w][:, a, :], in0=vector_head(w, h), scalar=vector_weight(w, a, h),
                    in1=vector_mix[w][:, a, :], op0=ALU.mult, op1=ALU.add,
                )

        def vector_measure(w, heads):
            if w not in vector_sumsq:
                vector_sumsq[w] = stage.tile([P, H], F32, name="vector_sumsq")
            squares_of(vector_mix[w], vector_sumsq[w], heads)

        def vector_normalise(w):
            i = vector_tile(w)
            inv_wide = inverse_rms(vector_sumsq[w], H)[:].unsqueeze(2).to_broadcast([P, H, HD])
            r[i] = stage.tile([P, H, HD], BF16, name="r", bufs=4)
            nc.gpsimd.tensor_tensor(out=r[i][:], in0=vector_mix[w][:], in1=inv_wide, op=ALU.mult)

        def transpose_r(i):
            r_t = psum.tile([P, H * P], BF16, tag="misc")
            assert is_vector(i) or (i, 1) in normalised
            for s in range(H):
                nc.tensor.transpose(r_t[:, s * P : (s + 1) * P], r[i][:, s, :], ident_bf16[:])
            if is_vector(i):
                by_pass = r_t[:].rearrange("p (q j t) -> p q t j", q=2, j=PACK)
            else:
                by_pass = r_t[:].rearrange("p (t q j) -> p q t j", q=2, j=PACK)
            r_grouped[i] = stage.tile([P, 2, P, PACK], BF16, align_bytes=64, name="r_grouped", bufs=3)
            copy = nc.vector.tensor_copy if i >= N_TILES - 3 else nc.scalar.copy
            copy(out=r_grouped[i][:], in_=by_pass)

        def quantise_r(i):
            codes = stage.tile([P, 2 * P], U32, align_bytes=64, name="r_codes", bufs=3)
            scales = stage.tile([P, 2 * P], U8, align_bytes=64, name="r_scales", bufs=3)
            nc.vector.quantize_mx(
                out=codes[:].bitcast(FP8X4), scales=scales[:], in_=r_grouped[i][:].rearrange("p q t j -> p (q t j)")
            )
            r_codes[i] = (codes, scales)

        def project_out(i):
            codes, scales = r_codes[i]
            acc[i] = psum.tile([P, C], F32, tag="misc", name="acc")
            for g in range(2):
                tok = slice(g * P, (g + 1) * P)
                nc.tensor.matmul_mx(
                    out=acc[i][:],
                    lhsT=codes[:, tok].bitcast(FP8X4),
                    lhsT_scale=scales[:, tok],
                    rhs=wo_codes[:, g * C : (g + 1) * C].bitcast(FP8X4),
                    rhs_scale=wo_scales[:, g * C : (g + 1) * C],
                    start=(g == 0),
                    stop=(g == 1),
                )

        def add_bias(i):
            out_sb[i] = stage.tile([P, C], F32, name="out_sb", bufs=4)
            nc.vector.tensor_tensor(out=out_sb[i][:], in0=acc[i][:], in1=bias[:], op=ALU.add)

        def store_out(i):
            nc.sync.dma_start(out=out_rows[i * P : (i + 1) * P, :], in_=out_sb[i][:])

        HALVES = (range(H // 2), range(H // 2, H))
        MIX_LAG = 3
        LAST_SLOT = N_TENSOR + 0
        STEPS = [
            (w, h, sums)
            for w in range(N_VECTOR)
            for h in (6, 4, 5, 0, 1, 2, 3)
            for sums in HALVES
        ]
        FIRST_STEPS = 4
        done = []
        started = []
        extra = []
        taken = []
        to_fill = []
        to_transpose = {}
        to_quantise = {}
        to_project = {}
        to_store = {}

        def plan(i, k):
            to_transpose.setdefault(k, []).append(i)
            to_quantise.setdefault(k + 1, []).append(i)
            to_project.setdefault(k + 2, []).append(i)
            to_store.setdefault(k + 3, []).append(i)

        for k in range(N_TENSOR):
            plan(tensor_tile(k), k + MIX_LAG + 1)

        def steps_due(k):
            if k < MIX_LAG:
                return FIRST_STEPS if k == MIX_LAG - 1 else 0
            late = (len(STEPS) - FIRST_STEPS) * (k + 1 - MIX_LAG)
            return min(FIRST_STEPS + late // (LAST_SLOT + 1 - MIX_LAG), len(STEPS))

        def work_on_extra(pieces, k):
            for piece in extra[len(taken) : len(taken) + pieces]:
                taken.append(piece)
                piece(k)

        def multiply(w, sums):
            def piece(k):
                vector_products(w, sums)
                if sums[-1] == H - 1:
                    started.append(w)
            return piece

        def measure_half(w, heads):
            def piece(k):
                vector_measure(w, heads)
            return piece

        def finish(w):
            def piece(k):
                vector_normalise(w)
                plan(vector_tile(w), k + 1)
            return piece

        def fill_banks():
            for w, bank in to_fill:
                vector_project(w, bank)
                if bank == 1:
                    for sums in HALVES:
                        extra.append(multiply(w, sums))
            to_fill.clear()

        def step(k):
            w, h, sums = STEPS[len(done)]
            while len(started) <= w:
                assert len(taken) < len(extra)
                work_on_extra(1, k)
            if (w, h // HEADS_PER_BANK) not in vector_v:
                fill_banks()
            vector_add_head(w, h, sums)
            done.append((w, h, sums))
            if sums[-1] == H - 1 and h == 5 and w + 1 < N_VECTOR:
                to_fill.append((w + 1, 1))
            if sums[-1] == H - 1 and h == 3:
                if w + 1 < N_VECTOR:
                    to_fill.append((w + 1, 0))
                for heads in HALVES:
                    extra.append(measure_half(w, heads))
                extra.append(finish(w))

        def is_slot(k):
            return 0 <= k < N_TENSOR

        def slot(k):
            if is_slot(k - MIX_LAG):
                mix_on_tensor(k - MIX_LAG, 0)
                measure(k - MIX_LAG, 0)
            q_next, step_next = divmod(k + 3, TENSOR_TILES)
            if step_next < QUAD // PAIR and 2 <= q_next < N_QUADS:
                transpose_x(q_next, step_next)
            if is_slot(k):
                project_and_spread(k)
            if is_slot(k - MIX_LAG):
                invert(k - MIX_LAG, 0)
            if is_slot(k - MIX_LAG - 1):
                normalise(k - MIX_LAG - 1, 1)
            for i in to_store.get(k, []):
                store_out(i)
            if k % TENSOR_TILES == 0 and k // TENSOR_TILES + 2 < N_QUADS:
                load_x(k // TENSOR_TILES + 2)
            if step_next == QUAD // PAIR and 2 <= q_next < N_QUADS:
                quantise_x(q_next)
            for i in to_quantise.get(k, []):
                quantise_r(i)
            work_on_extra(2, k)
            if is_slot(k - MIX_LAG):
                mix_on_tensor(k - MIX_LAG, 1)
                normalise(k - MIX_LAG, 0)
            if k % TENSOR_TILES == 1 and k // TENSOR_TILES + 1 < N_QUADS:
                lay_squares(k // TENSOR_TILES + 1)
            if k % TENSOR_TILES == 2 and k // TENSOR_TILES + 1 < N_QUADS:
                build_blocks(k // TENSOR_TILES + 1)
            if is_slot(k - MIX_LAG):
                measure(k - MIX_LAG, 1)
            fill_banks()
            for i in to_project.get(k, []):
                project_out(i)
                add_bias(i)
            for i in to_transpose.get(k, []):
                transpose_r(i)
            if is_slot(k - MIX_LAG):
                invert(k - MIX_LAG, 1)
            while len(done) < steps_due(k):
                step(k)

        WO_SLOT = 2
        load_wv(0)
        load_x(0)
        load_wv(1)
        load_vector_diff()
        load_diff_groups(0)
        load_x(1)
        load_wo()
        load_diff_groups(1)
        load_x(2)
        make_constants()
        transpose_wv(0)
        transpose_wv(1)
        transpose_x(0, 0)
        transpose_x(0, 1)
        quantise_wv(0)
        quantise_x(0)
        transpose_wv(2)
        transpose_wv(3)
        quantise_wv(1)
        project_and_spread(0)
        sort_diff(0)
        turn_diff(0)
        nc.vector.tensor_copy(out=vector_diff[:], in_=vector_diff_raw[:])
        lay_squares(0)
        build_blocks(0)
        project_and_spread(1)
        to_fill.append((0, 1))
        fill_banks()
        work_on_extra(2, 0)
        project_and_spread(2)
        to_fill.append((0, 0))
        fill_banks()
        transpose_x(1, 0)
        transpose_x(1, 1)
        while len(done) < FIRST_STEPS // 2:
            step(0)
        quantise_x(1)
        while len(done) < FIRST_STEPS:
            step(0)
        sort_diff(1)
        for k in range(MIX_LAG - 1, LAST_SLOT + 12):
            if k >= MIX_LAG:
                slot(k)
            else:
                lay_squares(1)
                build_blocks(1)
            if 0 <= k - WO_SLOT < C // P:
                transpose_wo(k - WO_SLOT)
            if k == WO_SLOT + C // P - 1:
                quantise_wo()
            if k == 6:
                turn_diff(1)
        assert len(taken) == len(extra) and len(done) == len(STEPS)
